import numpy as np
import ml_dtypes


def mxq(x, axis, fmt="e4m3"):
    dtype, down = {"e4m3": (ml_dtypes.float8_e4m3fn, 7), "e5m2": (ml_dtypes.float8_e5m2, 14)}[fmt]
    v = np.moveaxis(np.asarray(x, np.float32).astype(ml_dtypes.bfloat16).astype(np.float64), axis, -1)
    blocks = v.reshape(v.shape[:-1] + (-1, 32))
    amax = np.abs(blocks).max(-1, keepdims=True)
    byte = np.maximum(np.where(amax > 0, np.frexp(amax)[1] - 1 + 127, 0) - down, 1)
    scale = np.exp2(byte - 127.0)
    codes = (blocks / scale).astype(np.float32).astype(dtype).astype(np.float64)
    return np.moveaxis((codes * scale).reshape(v.shape), -1, axis)


WIDE = False


def mx_kscale(k):
    if not WIDE:
        return np.ones(k)
    levels = np.array([10, -10, 5, -5, 0])
    a = np.random.permutation(np.resize(levels, k // 512 * 4)).reshape(k // 512, 4)
    idx = np.arange(k)
    return np.exp2(a[idx // 512, idx % 128 // 32])


BF16 = ml_dtypes.bfloat16


def bf(x):
    return np.asarray(x, np.float32).astype(BF16)


def f64(x):
    return np.asarray(x).astype(np.float64)


E2M1 = np.array([0.0, 0.5, 1.0, 1.5, 2.0, 3.0, 4.0, 6.0, -0.0, -0.5, -1.0, -1.5, -2.0, -3.0, -4.0, -6.0])


def pack_weight(w, fmt):
    k, n = w.shape
    w = f64(bf(w)).reshape(k // 32, 32, n)
    amax = np.abs(w).max(1)
    if fmt == "e4m3":
        byte = np.frexp(amax)[1] - 1 + 127 - 7
    else:
        mant, ex = np.frexp(amax / 6.0)
        byte = np.where(mant > 0.5, ex, ex - 1) + 127
    byte = np.clip(np.where(amax > 0, byte, 1), 1, 254)
    scaled = (w * np.exp2(127.0 - byte)[:, None, :]).reshape(k, n).astype(np.float32)
    by_word = np.ascontiguousarray(scaled.reshape(k // 512, 128, 4, n).transpose(0, 1, 3, 2))
    if fmt == "e4m3":
        words = by_word.astype(ml_dtypes.float8_e4m3fn).view(np.uint8)
    else:
        c = by_word.astype(ml_dtypes.float4_e2m1fn).view(np.uint8) & 0xF
        words = c[..., 0::2] | (c[..., 1::2] << 4)
    return np.ascontiguousarray(words), np.ascontiguousarray(byte.astype(np.uint8).reshape(k // 512, 16, n))


def unpack_weight(words, scales, fmt):
    g, p, n, _ = words.shape
    if fmt == "e4m3":
        vals = np.ascontiguousarray(words).view(ml_dtypes.float8_e4m3fn).astype(np.float64)
    else:
        nib = np.empty((g, p, n, 4), np.uint8)
        nib[..., 0::2] = words & 0xF
        nib[..., 1::2] = words >> 4
        vals = E2M1[nib]
    vals = vals * np.repeat(np.exp2(scales.astype(np.float64) - 127.0), 8, axis=1)[..., None]
    return vals.transpose(0, 1, 3, 2).reshape(g * 512, n)


B, S, D_IN, MID, FFN, D_OUT, R = 2, 512, 256, 1024, 4096, 512, 16
LN_EPS = 1e-5
FMT = "e4m3"


def silu(v):
    return v / (1.0 + np.exp(-v))


def layer_norm(x, gamma, beta):
    m = np.mean(x, axis=-1, keepdims=True)
    v = np.mean(np.square(x - m), axis=-1, keepdims=True)
    return (x - m) / np.sqrt(v + LN_EPS) * gamma + beta


def setup_inputs():
    t, s = mx_kscale(FFN), mx_kscale(MID)
    h = bf(silu(np.random.standard_normal((B, S, FFN))) * t)
    w_f2 = np.random.standard_normal((MID, FFN)) / np.sqrt(FFN) / t
    b_f2 = bf(0.1 * np.random.standard_normal(MID))
    res1 = bf(0.7 * np.random.standard_normal((B, S, MID)))
    g2 = bf((1.0 + 0.1 * np.random.standard_normal(MID)) * s)
    be2 = bf(0.1 * np.random.standard_normal(MID) * s)
    w_h = np.random.standard_normal((D_OUT, MID)) / np.sqrt(MID) / s
    b_h = bf(0.1 * np.random.standard_normal(D_OUT))
    w_f2_words, w_f2_scales = pack_weight(np.ascontiguousarray(w_f2.T), FMT)
    w_h_words, w_h_scales = pack_weight(np.ascontiguousarray(w_h.T), FMT)
    return {"h": h,
            "w_f2_words": w_f2_words,
            "w_f2_scales": w_f2_scales,
            "b_f2": b_f2,
            "res1": res1,
            "g2": g2,
            "be2": be2,
            "w_h_words": w_h_words,
            "w_h_scales": w_h_scales,
            "b_h": b_h}


def reference(h, w_f2_words, w_f2_scales, b_f2, res1, g2, be2, w_h_words, w_h_scales, b_h):
    ffn = (mxq(f64(h), 2, "e4m3") @ unpack_weight(w_f2_words, w_f2_scales, FMT)) + f64(b_f2)
    res2 = f64(res1) + ffn
    norm2 = layer_norm(res2, f64(g2), f64(be2))
    return (mxq(norm2, 2, "e4m3") @ unpack_weight(w_h_words, w_h_scales, FMT)) + f64(b_h)

@@ -1,0 +1,337 @@
+from contextlib import ExitStack
+
+import concourse.mybir as mybir
+from concourse.masks import make_identity
+
+F32 = mybir.dt.float32
+BF16 = mybir.dt.bfloat16
+I32 = mybir.dt.int32
+U32 = mybir.dt.uint32
+U8 = mybir.dt.uint8
+FP8X4 = mybir.dt.float8_e4m3fn_x4
+ALU = mybir.AluOpType
+ACT = mybir.ActivationFunctionType
+
+P = 128
+PACK = 4
+K_PASS = P * PACK
+BANK = 512
+TOKENS = 1024
+FFN = 4096
+MID = 1024
+D_OUT = 512
+LN_EPS = 1e-5
+N_TILES = TOKENS // P
+FFN_PASSES = FFN // K_PASS
+MID_PASSES = MID // K_PASS
+PLANES_PER_TILE = 4
+
+FLOPS = 2 * TOKENS * FFN * MID + 2 * TOKENS * MID * D_OUT
+
+
+def tile_tsh_mid_block_pb_kernel(
+    tc, h, w_f2_words, w_f2_scales, b_f2, res1, g2, be2, w_h_words, w_h_scales, b_h, out
+):
+    nc = tc.nc
+    h_rows = h.flatten_outer_dims()
+    res1_rows = res1.flatten_outer_dims()
+    out_rows = out.flatten_outer_dims()
+
+    with ExitStack() as ctx:
+        ctx.enter_context(tc.manual_schedule())
+        keep = ctx.enter_context(tc.tile_pool(name="keep", bufs=1))
+        work = ctx.enter_context(tc.tile_pool(name="work", bufs=2))
+        acc_pool = ctx.enter_context(tc.psum_pool(name="acc", bufs=2))
+        ring = ctx.enter_context(tc.psum_pool(name="ring", bufs=6))
+
+        w_f2_planes = keep.tile([P, FFN_PASSES // PLANES_PER_TILE, MID], U8, align_bytes=64)
+        nc.vector.memset(w_f2_planes[:].rearrange("q a n -> q (a n)").bitcast(I32), 0)
+        w_h_planes = keep.tile([P, D_OUT], U8, align_bytes=64)
+        nc.vector.memset(w_h_planes[:].bitcast(I32), 0)
+        vector_row = keep.tile([P, 3 * MID + D_OUT], BF16)
+        nc.vector.memset(vector_row[:].bitcast(I32), 0)
+        ones = keep.tile([P, P], BF16)
+        nc.vector.memset(ones[:], 1.0)
+        eps = keep.tile([P, 1], F32)
+        nc.vector.memset(eps[:], LN_EPS)
+        ident_f32 = keep.tile([P, P], F32)
+        make_identity(nc, ident_f32[:])
+        ident_bf16 = keep.tile([P, P], BF16)
+        make_identity(nc, ident_bf16[:])
+
+        for v, vector in enumerate((b_f2, g2, be2)):
+            nc.scalar.dma_start(out=vector_row[0:1, v * MID : (v + 1) * MID], in_=vector.unsqueeze(0))
+        nc.scalar.dma_start(out=vector_row[0:1, 3 * MID :], in_=b_h.unsqueeze(0))
+
+        h_sb = []
+        res1_sb = []
+        for j in range(N_TILES):
+            h_tile = keep.tile([P, FFN], BF16, name="h%d" % j)
+            h_sb.append(h_tile)
+            res1_tile = keep.tile([P, MID], BF16, name="res1_%d" % j)
+            res1_sb.append(res1_tile)
+        w_f2_sb = keep.tile([P, FFN_PASSES, MID], U32, align_bytes=64)
+        w_h_sb = keep.tile([P, MID_PASSES, D_OUT], U32, align_bytes=64)
+
+        def load_h(j):
+            nc.sync.dma_start(out=h_sb[j][:], in_=h_rows[j * P : (j + 1) * P, :])
+
+        def load_res1(j):
+            nc.sync.dma_start(out=res1_sb[j][:], in_=res1_rows[j * P : (j + 1) * P, :])
+
+        def load_w_f2(half):
+            for g in range(FFN_PASSES):
+                nc.sync.dma_start(
+                    out=w_f2_sb[:, g, half * BANK : (half + 1) * BANK].bitcast(I32),
+                    in_=w_f2_words[g]
+                    .rearrange("p n t -> p (n t)")[:, half * BANK * PACK : (half + 1) * BANK * PACK]
+                    .bitcast(I32),
+                )
+
+        load_h(0)
+        load_h(1)
+        for a in range(FFN_PASSES // PLANES_PER_TILE):
+            for quadrant in range(4):
+                nc.sync.dma_start(
+                    out=w_f2_planes[32 * quadrant : 32 * quadrant + 16, a, :].bitcast(I32),
+                    in_=w_f2_scales[
+                        PLANES_PER_TILE * a : PLANES_PER_TILE * (a + 1), 4 * quadrant : 4 * quadrant + 4, :
+                    ].bitcast(I32),
+                )
+        load_w_f2(0)
+        load_res1(0)
+        load_w_f2(1)
+        load_res1(1)
+        load_h(2)
+        nc.sync.dma_start(
+            out=w_h_sb[:].bitcast(I32), in_=w_h_words.rearrange("g p n t -> p g (n t)").bitcast(I32)
+        )
+        for quadrant in range(4):
+            nc.sync.dma_start(
+                out=w_h_planes[32 * quadrant : 32 * quadrant + 4 * MID_PASSES, :].bitcast(I32),
+                in_=w_h_scales[:, 4 * quadrant : 4 * quadrant + 4, :].bitcast(I32),
+            )
+        for j in range(2, N_TILES):
+            load_res1(j)
+            if j + 1 < N_TILES:
+                load_h(j + 1)
+
+        bias_f2 = keep.tile([P, MID_PASSES, PACK, P], BF16)
+        gain = keep.tile([P, MID_PASSES, PACK, P], BF16)
+        shift = keep.tile([P, MID_PASSES, PACK, P], BF16)
+        bias_h = keep.tile([P, D_OUT], BF16)
+
+        def spread_vectors():
+            for v, spread in enumerate((bias_f2, gain, shift)):
+                for g in range(MID_PASSES):
+                    bank = ring.tile([P, BANK], F32, tag="ring")
+                    first = (MID_PASSES * v + g) * BANK
+                    nc.tensor.matmul(
+                        bank[:], lhsT=ones[:], rhs=vector_row[:, first : first + BANK], start=True, stop=True
+                    )
+                    nc.vector.tensor_copy(
+                        out=spread[:, g], in_=bank[:].rearrange("q (p t) -> q t p", t=PACK)
+                    )
+            bank = ring.tile([P, BANK], F32, tag="ring")
+            nc.tensor.matmul(bank[:], lhsT=ones[:], rhs=vector_row[:, 3 * MID :], start=True, stop=True)
+            nc.vector.tensor_copy(out=bias_h[:], in_=bank[:])
+
+        h_codes = {}
+        h_planes = {}
+
+        def quantise_h(j):
+            words = h_sb[j][:].bitcast(F32)
+            grouped = work.tile([P, FFN], BF16, align_bytes=64, tag="h_grouped")
+            grouped_words = grouped[:].bitcast(F32).rearrange("q (g c u) -> q g c u", g=FFN_PASSES, u=2)
+            codes = work.tile([P, FFN_PASSES * P], U32, align_bytes=64, tag="h_codes")
+            planes = work.tile([P, FFN_PASSES * P], U8, align_bytes=64, tag="h_planes")
+            for b in range(FFN_PASSES // 2):
+                bank = ring.tile([P, 2, 2, P], F32, tag="ring")
+                for gg in range(2):
+                    for u in range(2):
+                        first = (K_PASS // 2) * (2 * b + gg)
+                        nc.tensor.transpose(
+                            bank[:, gg, u, :], words[:, first + u : first + K_PASS // 2 : 2], ident_f32[:]
+                        )
+                nc.scalar.copy(
+                    out=grouped_words[:, 2 * b : 2 * b + 2, :, :],
+                    in_=bank[:].rearrange("q g u c -> q g c u"),
+                )
+            for a in range(2):
+                nc.vector.quantize_mx(
+                    out=codes[:, a * 512 : (a + 1) * 512].bitcast(FP8X4),
+                    scales=planes[:, a * 512 : (a + 1) * 512],
+                    in_=grouped[:, a * 2048 : (a + 1) * 2048],
+                )
+            h_codes[j] = codes
+            h_planes[j] = planes
+
+        res1_biased = {}
+
+        def add_bias_to_residual(j):
+            biased = work.tile([P, MID_PASSES, PACK, P], F32, tag="res1_biased")
+            nc.vector.tensor_tensor(
+                out=biased[:],
+                in0=res1_sb[j][:].rearrange("q (g p t) -> q g t p", g=MID_PASSES, t=PACK),
+                in1=bias_f2[:],
+                op=ALU.add,
+            )
+            res1_biased[j] = biased
+
+        acc = {}
+        res2 = {}
+        row_sums = {}
+
+        def first_matmul(j, half):
+            bank = acc_pool.tile([P, BANK], F32, tag="acc")
+            for g in range(FFN_PASSES):
+                plane = PACK * (g % PLANES_PER_TILE)
+                nc.tensor.matmul_mx(
+                    out=bank[:],
+                    lhsT=h_codes[j][:, g * P : (g + 1) * P].bitcast(FP8X4),
+                    lhsT_scale=h_planes[j][:, g * P : (g + 1) * P],
+                    rhs=w_f2_sb[:, g, half * BANK : (half + 1) * BANK].bitcast(FP8X4),
+                    rhs_scale=w_f2_planes[plane:P, g // PLANES_PER_TILE, half * BANK : (half + 1) * BANK],
+                    start=(g == 0),
+                    stop=(g == FFN_PASSES - 1),
+                )
+            acc[(j, half)] = bank
+
+        def add_residual(j, half):
+            if half == 0:
+                res2_tile = work.tile([P, MID_PASSES, PACK, P], F32, tag="res2")
+                res2[j] = res2_tile
+                sums = work.tile([P, MID_PASSES], F32, tag="row_sums", bufs=3)
+                row_sums[j] = sums
+            nc.vector.scalar_tensor_tensor(
+                out=res2[j][:, half],
+                in0=acc[(j, half)][:].rearrange("q (p t) -> q t p", t=PACK),
+                scalar=1.0,
+                in1=res1_biased[j][:, half],
+                op0=ALU.mult,
+                op1=ALU.add,
+                accum_out=row_sums[j][:, half : half + 1],
+            )
+
+        minus_mean = {}
+        norm2 = {}
+
+        def mean(j):
+            negative = work.tile([P, 1], F32, tag="minus_mean", bufs=3)
+            nc.vector.tensor_scalar(
+                out=negative[:],
+                in0=row_sums[j][:, 0:1],
+                scalar1=row_sums[j][:, 1:2],
+                scalar2=-1.0 / MID,
+                op0=ALU.add,
+                op1=ALU.mult,
+            )
+            minus_mean[j] = negative
+
+        def layer_norm(j):
+            squares = work.tile([P, MID], BF16, tag="squares")
+            sum_squares = work.tile([P, 1], F32, tag="sum_squares")
+            nc.scalar.activation(
+                out=squares[:],
+                in_=res2[j][:].rearrange("q g t p -> q (g t p)"),
+                func=ACT.Square,
+                bias=minus_mean[j][:, 0:1],
+                scale=1.0,
+                accum_out=sum_squares[:, 0:1],
+            )
+            std = work.tile([P, 1], F32, tag="std")
+            nc.scalar.activation(
+                out=std[:], in_=sum_squares[:], func=ACT.Sqrt, bias=eps[:, 0:1], scale=1.0 / MID
+            )
+            rstd = work.tile([P, 1], F32, tag="rstd")
+            nc.vector.reciprocal(out=rstd[:], in_=std[:])
+            gained = work.tile([P, MID_PASSES, PACK * P], F32, tag="gained")
+            normed = work.tile([P, MID_PASSES, PACK * P], BF16, tag="norm2")
+            for g in range(MID_PASSES):
+                nc.vector.scalar_tensor_tensor(
+                    out=gained[:, g],
+                    in0=res2[j][:, g].rearrange("q t p -> q (t p)"),
+                    scalar=minus_mean[j][:, 0:1],
+                    in1=gain[:, g].rearrange("q t p -> q (t p)"),
+                    op0=ALU.add,
+                    op1=ALU.mult,
+                )
+            for g in range(MID_PASSES):
+                nc.vector.scalar_tensor_tensor(
+                    out=normed[:, g],
+                    in0=gained[:, g],
+                    scalar=rstd[:, 0:1],
+                    in1=shift[:, g].rearrange("q t p -> q (t p)"),
+                    op0=ALU.mult,
+                    op1=ALU.add,
+                )
+            norm2[j] = normed
+
+        norm2_codes = {}
+        norm2_planes = {}
+
+        def quantise_norm2(j):
+            bank = ring.tile([P, MID_PASSES * PACK, P], BF16, tag="ring")
+            columns = norm2[j][:].rearrange("q g n -> q (g n)")
+            for gt in range(MID_PASSES * PACK):
+                nc.tensor.transpose(bank[:, gt, :], columns[:, gt * P : (gt + 1) * P], ident_bf16[:])
+            grouped = work.tile([P, MID_PASSES, P, PACK], BF16, align_bytes=64, tag="norm2_grouped")
+            nc.scalar.copy(out=grouped[:], in_=bank[:].rearrange("q (g t) c -> q g c t", g=MID_PASSES))
+            codes = work.tile([P, MID_PASSES * P], U32, align_bytes=64, tag="norm2_codes")
+            planes = work.tile([P, MID_PASSES * P], U8, align_bytes=64, tag="norm2_planes")
+            nc.vector.quantize_mx(
+                out=codes[:].bitcast(FP8X4),
+                scales=planes[:],
+                in_=grouped[:].rearrange("q g c t -> q (g c t)"),
+            )
+            norm2_codes[j] = codes
+            norm2_planes[j] = planes
+
+        product = {}
+
+        def second_matmul(j):
+            bank = ring.tile([P, D_OUT], F32, tag="ring")
+            for g in range(MID_PASSES):
+                nc.tensor.matmul_mx(
+                    out=bank[:],
+                    lhsT=norm2_codes[j][:, g * P : (g + 1) * P].bitcast(FP8X4),
+                    lhsT_scale=norm2_planes[j][:, g * P : (g + 1) * P],
+                    rhs=w_h_sb[:, g, :].bitcast(FP8X4),
+                    rhs_scale=w_h_planes[PACK * g : P, :],
+                    start=(g == 0),
+                    stop=(g == MID_PASSES - 1),
+                )
+            product[j] = bank
+
+        def store(j):
+            result = work.tile([P, D_OUT], F32, tag="result", bufs=3)
+            nc.vector.tensor_tensor(out=result[:], in0=product[j][:], in1=bias_h[:], op=ALU.add)
+            nc.sync.dma_start(out=out_rows[j * P : (j + 1) * P, :], in_=result[:])
+
+        def live(j):
+            return 0 <= j < N_TILES
+
+        quantise_h(0)
+        spread_vectors()
+        add_bias_to_residual(0)
+        for i in range(N_TILES + 3):
+            if live(i - 1):
+                add_residual(i - 1, 1)
+                mean(i - 1)
+            if live(i - 3):
+                store(i - 3)
+            if live(i + 1):
+                quantise_h(i + 1)
+            if live(i - 2):
+                quantise_norm2(i - 2)
+            if live(i + 1):
+                add_bias_to_residual(i + 1)
+            if live(i):
+                first_matmul(i, 0)
+                add_residual(i, 0)
+            if live(i - 1):
+                layer_norm(i - 1)
+            if live(i):
+                first_matmul(i, 1)
+            if live(i - 2):
+                second_matmul(i - 2)

@@ -136,11 +136,18 @@ def tile_tsh_mid_block_pb_kernel(
             nc.tensor.matmul(bank[:], lhsT=ones[:], rhs=vector_row[:, 3 * MID :], start=True, stop=True)
             nc.vector.tensor_copy(out=bias_h[:], in_=bank[:])
 
+        h_sorted = {}
         h_codes = {}
         h_planes = {}
 
+        def sort_h(j):
+            words = h_sb[j][:].bitcast(F32).rearrange("q (g p u) -> q g u p", g=FFN_PASSES, u=2)
+            ordered = work.tile([P, FFN_PASSES, 2, P], F32, tag="h_sorted")
+            for b in range(FFN_PASSES // 2):
+                nc.scalar.copy(out=ordered[:, 2 * b : 2 * b + 2], in_=words[:, 2 * b : 2 * b + 2])
+            h_sorted[j] = ordered
+
         def quantise_h(j):
-            words = h_sb[j][:].bitcast(F32)
             grouped = work.tile([P, FFN], BF16, align_bytes=64, tag="h_grouped")
             grouped_words = grouped[:].bitcast(F32).rearrange("q (g c u) -> q g c u", g=FFN_PASSES, u=2)
             codes = work.tile([P, FFN_PASSES * P], U32, align_bytes=64, tag="h_codes")
@@ -149,10 +156,7 @@ def tile_tsh_mid_block_pb_kernel(
                 bank = ring.tile([P, 2, 2, P], F32, tag="ring")
                 for gg in range(2):
                     for u in range(2):
-                        first = (K_PASS // 2) * (2 * b + gg)
-                        nc.tensor.transpose(
-                            bank[:, gg, u, :], words[:, first + u : first + K_PASS // 2 : 2], ident_f32[:]
-                        )
+                        nc.tensor.transpose(bank[:, gg, u, :], h_sorted[j][:, 2 * b + gg, u, :], ident_f32[:])
                 nc.scalar.copy(
                     out=grouped_words[:, 2 * b : 2 * b + 2, :, :],
                     in_=bank[:].rearrange("q g u c -> q g c u"),
@@ -311,9 +315,11 @@ def tile_tsh_mid_block_pb_kernel(
         def live(j):
             return 0 <= j < N_TILES
 
+        sort_h(0)
         quantise_h(0)
         spread_vectors()
         add_bias_to_residual(0)
+        sort_h(1)
         for i in range(N_TILES + 3):
             if live(i - 1):
                 add_residual(i - 1, 1)
@@ -331,6 +337,8 @@ def tile_tsh_mid_block_pb_kernel(
                 add_residual(i, 0)
             if live(i - 1):
                 layer_norm(i - 1)
+            if live(i + 2):
+                sort_h(i + 2)
             if live(i):
                 first_matmul(i, 1)
             if live(i - 2):

@@ -88,8 +88,8 @@ def tile_tsh_mid_block_pb_kernel(
                     .bitcast(I32),
                 )
 
-        load_h(0)
-        load_h(1)
+        for j in range(3):
+            load_h(j)
         for a in range(FFN_PASSES // PLANES_PER_TILE):
             for quadrant in range(4):
                 nc.sync.dma_start(
@@ -99,10 +99,10 @@ def tile_tsh_mid_block_pb_kernel(
                     ].bitcast(I32),
                 )
         load_w_f2(0)
-        load_res1(0)
+        for j in range(3):
+            load_res1(j)
         load_w_f2(1)
-        load_res1(1)
-        load_h(2)
+        load_h(3)
         nc.sync.dma_start(
             out=w_h_sb[:].bitcast(I32), in_=w_h_words.rearrange("g p n t -> p g (n t)").bitcast(I32)
         )
@@ -111,7 +111,7 @@ def tile_tsh_mid_block_pb_kernel(
                 out=w_h_planes[32 * quadrant : 32 * quadrant + 4 * MID_PASSES, :].bitcast(I32),
                 in_=w_h_scales[:, 4 * quadrant : 4 * quadrant + 4, :].bitcast(I32),
             )
-        for j in range(2, N_TILES):
+        for j in range(3, N_TILES):
             load_res1(j)
             if j + 1 < N_TILES:
                 load_h(j + 1)
@@ -136,36 +136,33 @@ def tile_tsh_mid_block_pb_kernel(
             nc.tensor.matmul(bank[:], lhsT=ones[:], rhs=vector_row[:, 3 * MID :], start=True, stop=True)
             nc.vector.tensor_copy(out=bias_h[:], in_=bank[:])
 
-        h_sorted = {}
+        h_grouped = {}
         h_codes = {}
         h_planes = {}
 
-        def sort_h(j):
+        def transpose_h(j):
             words = h_sb[j][:].bitcast(F32).rearrange("q (g p u) -> q g u p", g=FFN_PASSES, u=2)
-            ordered = work.tile([P, FFN_PASSES, 2, P], F32, tag="h_sorted")
-            for b in range(FFN_PASSES // 2):
-                nc.scalar.copy(out=ordered[:, 2 * b : 2 * b + 2], in_=words[:, 2 * b : 2 * b + 2])
-            h_sorted[j] = ordered
-
-        def quantise_h(j):
             grouped = work.tile([P, FFN], BF16, align_bytes=64, tag="h_grouped")
             grouped_words = grouped[:].bitcast(F32).rearrange("q (g c u) -> q g c u", g=FFN_PASSES, u=2)
-            codes = work.tile([P, FFN_PASSES * P], U32, align_bytes=64, tag="h_codes")
-            planes = work.tile([P, FFN_PASSES * P], U8, align_bytes=64, tag="h_planes")
             for b in range(FFN_PASSES // 2):
                 bank = ring.tile([P, 2, 2, P], F32, tag="ring")
                 for gg in range(2):
                     for u in range(2):
-                        nc.tensor.transpose(bank[:, gg, u, :], h_sorted[j][:, 2 * b + gg, u, :], ident_f32[:])
+                        nc.tensor.transpose(bank[:, gg, u, :], words[:, 2 * b + gg, u, :], ident_f32[:])
                 nc.scalar.copy(
                     out=grouped_words[:, 2 * b : 2 * b + 2, :, :],
                     in_=bank[:].rearrange("q g u c -> q g c u"),
                 )
+            h_grouped[j] = grouped
+
+        def quantise_h(j):
+            codes = work.tile([P, FFN_PASSES * P], U32, align_bytes=64, tag="h_codes", bufs=3)
+            planes = work.tile([P, FFN_PASSES * P], U8, align_bytes=64, tag="h_planes", bufs=3)
             for a in range(2):
                 nc.vector.quantize_mx(
                     out=codes[:, a * 512 : (a + 1) * 512].bitcast(FP8X4),
                     scales=planes[:, a * 512 : (a + 1) * 512],
-                    in_=grouped[:, a * 2048 : (a + 1) * 2048],
+                    in_=h_grouped[j][:, a * 2048 : (a + 1) * 2048],
                 )
             h_codes[j] = codes
             h_planes[j] = planes
@@ -173,7 +170,7 @@ def tile_tsh_mid_block_pb_kernel(
         res1_biased = {}
 
         def add_bias_to_residual(j):
-            biased = work.tile([P, MID_PASSES, PACK, P], F32, tag="res1_biased")
+            biased = work.tile([P, MID_PASSES, PACK, P], F32, tag="res1_biased", bufs=3)
             nc.vector.tensor_tensor(
                 out=biased[:],
                 in0=res1_sb[j][:].rearrange("q (g p t) -> q g t p", g=MID_PASSES, t=PACK),
@@ -250,7 +247,7 @@ def tile_tsh_mid_block_pb_kernel(
             rstd = work.tile([P, 1], F32, tag="rstd")
             nc.vector.reciprocal(out=rstd[:], in_=std[:])
             gained = work.tile([P, MID_PASSES, PACK * P], F32, tag="gained")
-            normed = work.tile([P, MID_PASSES, PACK * P], BF16, tag="norm2")
+            normed = work.tile([P, MID_PASSES, PACK * P], BF16, tag="norm2", bufs=3)
             for g in range(MID_PASSES):
                 nc.vector.scalar_tensor_tensor(
                     out=gained[:, g],
@@ -271,22 +268,28 @@ def tile_tsh_mid_block_pb_kernel(
                 )
             norm2[j] = normed
 
+        norm2_grouped = {}
         norm2_codes = {}
         norm2_planes = {}
 
-        def quantise_norm2(j):
+        def transpose_norm2(j):
             bank = ring.tile([P, MID_PASSES * PACK, P], BF16, tag="ring")
             columns = norm2[j][:].rearrange("q g n -> q (g n)")
             for gt in range(MID_PASSES * PACK):
                 nc.tensor.transpose(bank[:, gt, :], columns[:, gt * P : (gt + 1) * P], ident_bf16[:])
             grouped = work.tile([P, MID_PASSES, P, PACK], BF16, align_bytes=64, tag="norm2_grouped")
-            nc.scalar.copy(out=grouped[:], in_=bank[:].rearrange("q (g t) c -> q g c t", g=MID_PASSES))
+            by_pass = bank[:].rearrange("q (g t) c -> q g c t", g=MID_PASSES)
+            for g in range(MID_PASSES):
+                nc.scalar.copy(out=grouped[:, g], in_=by_pass[:, g])
+            norm2_grouped[j] = grouped
+
+        def quantise_norm2(j):
             codes = work.tile([P, MID_PASSES * P], U32, align_bytes=64, tag="norm2_codes")
             planes = work.tile([P, MID_PASSES * P], U8, align_bytes=64, tag="norm2_planes")
             nc.vector.quantize_mx(
                 out=codes[:].bitcast(FP8X4),
                 scales=planes[:],
-                in_=grouped[:].rearrange("q g c t -> q (g c t)"),
+                in_=norm2_grouped[j][:].rearrange("q g c t -> q (g c t)"),
             )
             norm2_codes[j] = codes
             norm2_planes[j] = planes
@@ -312,34 +315,39 @@ def tile_tsh_mid_block_pb_kernel(
             nc.vector.tensor_tensor(out=result[:], in0=product[j][:], in1=bias_h[:], op=ALU.add)
             nc.sync.dma_start(out=out_rows[j * P : (j + 1) * P, :], in_=result[:])
 
-        def live(j):
-            return 0 <= j < N_TILES
+        rounds = [(0, 1)] + [(j,) for j in range(2, N_TILES)]
 
-        sort_h(0)
-        quantise_h(0)
+        def tiles(r):
+            return rounds[r] if 0 <= r < len(rounds) else ()
+
+        for j in tiles(0):
+            transpose_h(j)
+            quantise_h(j)
         spread_vectors()
-        add_bias_to_residual(0)
-        sort_h(1)
-        for i in range(N_TILES + 3):
-            if live(i - 1):
-                add_residual(i - 1, 1)
-                mean(i - 1)
-            if live(i - 3):
-                store(i - 3)
-            if live(i + 1):
-                quantise_h(i + 1)
-            if live(i - 2):
-                quantise_norm2(i - 2)
-            if live(i + 1):
-                add_bias_to_residual(i + 1)
-            if live(i):
-                first_matmul(i, 0)
-                add_residual(i, 0)
-            if live(i - 1):
-                layer_norm(i - 1)
-            if live(i + 2):
-                sort_h(i + 2)
-            if live(i):
-                first_matmul(i, 1)
-            if live(i - 2):
-                second_matmul(i - 2)
+        for j in tiles(0):
+            add_bias_to_residual(j)
+        for r in range(len(rounds) + 3):
+            for j in tiles(r - 1):
+                add_residual(j, 1)
+                mean(j)
+            for j in tiles(r - 3):
+                store(j)
+            for j in tiles(r + 1):
+                add_bias_to_residual(j)
+            for j in tiles(r - 1):
+                layer_norm(j)
+            for j in tiles(r - 2):
+                transpose_norm2(j)
+            for j in tiles(r + 1):
+                transpose_h(j)
+            for j in tiles(r):
+                first_matmul(j, 0)
+                add_residual(j, 0)
+            for j in tiles(r - 2):
+                quantise_norm2(j)
+            for j in tiles(r + 1):
+                quantise_h(j)
+            for j in tiles(r):
+                first_matmul(j, 1)
+            for j in tiles(r - 2):
+                second_matmul(j)

@@ -25,6 +25,8 @@ N_TILES = TOKENS // P
 FFN_PASSES = FFN // K_PASS
 MID_PASSES = MID // K_PASS
 PLANES_PER_TILE = 4
+H_BUFFERS = 4
+FIRST_SORTED = 4
 
 FLOPS = 2 * TOKENS * FFN * MID + 2 * TOKENS * MID * D_OUT
 
@@ -41,6 +43,7 @@ def tile_tsh_mid_block_pb_kernel(
         ctx.enter_context(tc.manual_schedule())
         keep = ctx.enter_context(tc.tile_pool(name="keep", bufs=1))
         work = ctx.enter_context(tc.tile_pool(name="work", bufs=2))
+        h_pool = ctx.enter_context(tc.tile_pool(name="h", bufs=H_BUFFERS))
         acc_pool = ctx.enter_context(tc.psum_pool(name="acc", bufs=2))
         ring = ctx.enter_context(tc.psum_pool(name="ring", bufs=6))
 
@@ -63,21 +66,20 @@ def tile_tsh_mid_block_pb_kernel(
             nc.scalar.dma_start(out=vector_row[0:1, v * MID : (v + 1) * MID], in_=vector.unsqueeze(0))
         nc.scalar.dma_start(out=vector_row[0:1, 3 * MID :], in_=b_h.unsqueeze(0))
 
-        h_sb = []
-        res1_sb = []
-        for j in range(N_TILES):
-            h_tile = keep.tile([P, FFN], BF16, name="h%d" % j)
-            h_sb.append(h_tile)
-            res1_tile = keep.tile([P, MID], BF16, name="res1_%d" % j)
-            res1_sb.append(res1_tile)
+        h_sb = {}
+        res1_sb = {}
         w_f2_sb = keep.tile([P, FFN_PASSES, MID], U32, align_bytes=64)
         w_h_sb = keep.tile([P, MID_PASSES, D_OUT], U32, align_bytes=64)
 
         def load_h(j):
-            nc.sync.dma_start(out=h_sb[j][:], in_=h_rows[j * P : (j + 1) * P, :])
+            h_tile = h_pool.tile([P, FFN], BF16, tag="h")
+            nc.sync.dma_start(out=h_tile[:], in_=h_rows[j * P : (j + 1) * P, :])
+            h_sb[j] = h_tile
 
         def load_res1(j):
-            nc.sync.dma_start(out=res1_sb[j][:], in_=res1_rows[j * P : (j + 1) * P, :])
+            res1_tile = keep.tile([P, MID], BF16, name="res1_%d" % j)
+            nc.sync.dma_start(out=res1_tile[:], in_=res1_rows[j * P : (j + 1) * P, :])
+            res1_sb[j] = res1_tile
 
         def load_w_f2(half):
             for g in range(FFN_PASSES):
@@ -111,10 +113,7 @@ def tile_tsh_mid_block_pb_kernel(
                 out=w_h_planes[32 * quadrant : 32 * quadrant + 4 * MID_PASSES, :].bitcast(I32),
                 in_=w_h_scales[:, 4 * quadrant : 4 * quadrant + 4, :].bitcast(I32),
             )
-        for j in range(3, N_TILES):
-            load_res1(j)
-            if j + 1 < N_TILES:
-                load_h(j + 1)
+        load_res1(3)
 
         bias_f2 = keep.tile([P, MID_PASSES, PACK, P], BF16)
         gain = keep.tile([P, MID_PASSES, PACK, P], BF16)
@@ -140,8 +139,20 @@ def tile_tsh_mid_block_pb_kernel(
         h_codes = {}
         h_planes = {}
 
+        h_sorted = {}
+
+        def h_words(j):
+            return h_sb[j][:].bitcast(F32).rearrange("q (g p u) -> q g u p", g=FFN_PASSES, u=2)
+
+        def sort_h(j):
+            words = h_words(j)
+            ordered = work.tile([P, FFN_PASSES, 2, P], F32, tag="h_sorted")
+            for b in range(FFN_PASSES // 2):
+                nc.scalar.copy(out=ordered[:, 2 * b : 2 * b + 2], in_=words[:, 2 * b : 2 * b + 2])
+            h_sorted[j] = ordered
+
         def transpose_h(j):
-            words = h_sb[j][:].bitcast(F32).rearrange("q (g p u) -> q g u p", g=FFN_PASSES, u=2)
+            words = h_sorted[j][:] if j in h_sorted else h_words(j)
             grouped = work.tile([P, FFN], BF16, align_bytes=64, tag="h_grouped")
             grouped_words = grouped[:].bitcast(F32).rearrange("q (g c u) -> q g c u", g=FFN_PASSES, u=2)
             for b in range(FFN_PASSES // 2):
@@ -229,7 +240,10 @@ def tile_tsh_mid_block_pb_kernel(
             )
             minus_mean[j] = negative
 
-        def layer_norm(j):
+        rstd_input = {}
+        gained_rows = {}
+
+        def deviation(j):
             squares = work.tile([P, MID], BF16, tag="squares")
             sum_squares = work.tile([P, 1], F32, tag="sum_squares")
             nc.scalar.activation(
@@ -244,10 +258,10 @@ def tile_tsh_mid_block_pb_kernel(
             nc.scalar.activation(
                 out=std[:], in_=sum_squares[:], func=ACT.Sqrt, bias=eps[:, 0:1], scale=1.0 / MID
             )
-            rstd = work.tile([P, 1], F32, tag="rstd")
-            nc.vector.reciprocal(out=rstd[:], in_=std[:])
+            rstd_input[j] = std
+
+        def centre_and_gain(j):
             gained = work.tile([P, MID_PASSES, PACK * P], F32, tag="gained")
-            normed = work.tile([P, MID_PASSES, PACK * P], BF16, tag="norm2", bufs=3)
             for g in range(MID_PASSES):
                 nc.vector.scalar_tensor_tensor(
                     out=gained[:, g],
@@ -257,10 +271,16 @@ def tile_tsh_mid_block_pb_kernel(
                     op0=ALU.add,
                     op1=ALU.mult,
                 )
+            gained_rows[j] = gained
+
+        def scale_and_shift(j):
+            rstd = work.tile([P, 1], F32, tag="rstd")
+            nc.vector.reciprocal(out=rstd[:], in_=rstd_input[j][:])
+            normed = work.tile([P, MID_PASSES, PACK * P], BF16, tag="norm2", bufs=3)
             for g in range(MID_PASSES):
                 nc.vector.scalar_tensor_tensor(
                     out=normed[:, g],
-                    in0=gained[:, g],
+                    in0=gained_rows[j][:, g],
                     scalar=rstd[:, 0:1],
                     in1=shift[:, g].rearrange("q t p -> q (t p)"),
                     op0=ALU.mult,
@@ -327,19 +347,28 @@ def tile_tsh_mid_block_pb_kernel(
         for j in tiles(0):
             add_bias_to_residual(j)
         for r in range(len(rounds) + 3):
+            for j in tiles(r + 3):
+                load_h(j)
+                load_res1(j)
             for j in tiles(r - 1):
                 add_residual(j, 1)
                 mean(j)
+                deviation(j)
             for j in tiles(r - 3):
                 store(j)
+            for j in tiles(r - 1):
+                centre_and_gain(j)
             for j in tiles(r + 1):
                 add_bias_to_residual(j)
             for j in tiles(r - 1):
-                layer_norm(j)
+                scale_and_shift(j)
             for j in tiles(r - 2):
                 transpose_norm2(j)
             for j in tiles(r + 1):
                 transpose_h(j)
+            for j in tiles(r + 2):
+                if j >= FIRST_SORTED:
+                    sort_h(j)
             for j in tiles(r):
                 first_matmul(j, 0)
                 add_residual(j, 0)

@@ -25,7 +25,9 @@ N_TILES = TOKENS // P
 FFN_PASSES = FFN // K_PASS
 MID_PASSES = MID // K_PASS
 PLANES_PER_TILE = 4
-H_BUFFERS = 4
+H_BUFFERS = 6
+GP_BIAS = False
+PSUM_CONST = False
 FIRST_SORTED = 4
 
 FLOPS = 2 * TOKENS * FFN * MID + 2 * TOKENS * MID * D_OUT
@@ -45,22 +47,21 @@ def tile_tsh_mid_block_pb_kernel(
         work = ctx.enter_context(tc.tile_pool(name="work", bufs=2))
         h_pool = ctx.enter_context(tc.tile_pool(name="h", bufs=H_BUFFERS))
         acc_pool = ctx.enter_context(tc.psum_pool(name="acc", bufs=2))
-        ring = ctx.enter_context(tc.psum_pool(name="ring", bufs=6))
+        ring = ctx.enter_context(tc.psum_pool(name="ring", bufs=4 if PSUM_CONST else 6))
+        fixed = ctx.enter_context(tc.psum_pool(name="fixed", bufs=1)) if PSUM_CONST else None
 
         w_f2_planes = keep.tile([P, FFN_PASSES // PLANES_PER_TILE, MID], U8, align_bytes=64)
         nc.vector.memset(w_f2_planes[:].rearrange("q a n -> q (a n)").bitcast(I32), 0)
-        w_h_planes = keep.tile([P, D_OUT], U8, align_bytes=64)
-        nc.vector.memset(w_h_planes[:].bitcast(I32), 0)
         vector_row = keep.tile([P, 3 * MID + D_OUT], BF16)
         nc.vector.memset(vector_row[:].bitcast(I32), 0)
         ones = keep.tile([P, P], BF16)
         nc.vector.memset(ones[:], 1.0)
+        w_h_planes = keep.tile([P, D_OUT], U8, align_bytes=64)
+        nc.vector.memset(w_h_planes[:].bitcast(I32), 0)
         eps = keep.tile([P, 1], F32)
         nc.vector.memset(eps[:], LN_EPS)
         ident_f32 = keep.tile([P, P], F32)
         make_identity(nc, ident_f32[:])
-        ident_bf16 = keep.tile([P, P], BF16)
-        make_identity(nc, ident_bf16[:])
 
         for v, vector in enumerate((b_f2, g2, be2)):
             nc.scalar.dma_start(out=vector_row[0:1, v * MID : (v + 1) * MID], in_=vector.unsqueeze(0))
@@ -71,9 +72,14 @@ def tile_tsh_mid_block_pb_kernel(
         w_f2_sb = keep.tile([P, FFN_PASSES, MID], U32, align_bytes=64)
         w_h_sb = keep.tile([P, MID_PASSES, D_OUT], U32, align_bytes=64)
 
-        def load_h(j):
+        def load_h(j, pieces=1):
             h_tile = h_pool.tile([P, FFN], BF16, tag="h")
-            nc.sync.dma_start(out=h_tile[:], in_=h_rows[j * P : (j + 1) * P, :])
+            width = FFN // pieces
+            for c in range(pieces):
+                nc.sync.dma_start(
+                    out=h_tile[:, c * width : (c + 1) * width],
+                    in_=h_rows[j * P : (j + 1) * P, c * width : (c + 1) * width],
+                )
             h_sb[j] = h_tile
 
         def load_res1(j):
@@ -90,8 +96,18 @@ def tile_tsh_mid_block_pb_kernel(
                     .bitcast(I32),
                 )
 
-        for j in range(3):
-            load_h(j)
+        def load_w_h():
+            nc.sync.dma_start(
+                out=w_h_sb[:].bitcast(I32), in_=w_h_words.rearrange("g p n t -> p g (n t)").bitcast(I32)
+            )
+            for quadrant in range(4):
+                nc.sync.dma_start(
+                    out=w_h_planes[32 * quadrant : 32 * quadrant + 4 * MID_PASSES, :].bitcast(I32),
+                    in_=w_h_scales[:, 4 * quadrant : 4 * quadrant + 4, :].bitcast(I32),
+                )
+
+        for j in range(2):
+            load_h(j, 4)
         for a in range(FFN_PASSES // PLANES_PER_TILE):
             for quadrant in range(4):
                 nc.sync.dma_start(
@@ -101,44 +117,60 @@ def tile_tsh_mid_block_pb_kernel(
                     ].bitcast(I32),
                 )
         load_w_f2(0)
-        for j in range(3):
+        for j in range(2):
             load_res1(j)
         load_w_f2(1)
-        load_h(3)
-        nc.sync.dma_start(
-            out=w_h_sb[:].bitcast(I32), in_=w_h_words.rearrange("g p n t -> p g (n t)").bitcast(I32)
-        )
-        for quadrant in range(4):
-            nc.sync.dma_start(
-                out=w_h_planes[32 * quadrant : 32 * quadrant + 4 * MID_PASSES, :].bitcast(I32),
-                in_=w_h_scales[:, 4 * quadrant : 4 * quadrant + 4, :].bitcast(I32),
-            )
+        for j in range(2, 4):
+            load_h(j, 4)
+        load_res1(2)
+        load_h(4)
+        load_w_h()
         load_res1(3)
+        load_res1(4)
+        load_h(5)
+        load_res1(5)
 
-        bias_f2 = keep.tile([P, MID_PASSES, PACK, P], BF16)
-        gain = keep.tile([P, MID_PASSES, PACK, P], BF16)
-        shift = keep.tile([P, MID_PASSES, PACK, P], BF16)
+        bias_f2 = keep.tile([P, MID_PASSES, BANK], BF16)
         bias_h = keep.tile([P, D_OUT], BF16)
+        if PSUM_CONST:
+            gain = fixed.tile([P, MID_PASSES, BANK], BF16, name="gain")
+            shift = fixed.tile([P, MID_PASSES, BANK], BF16, name="shift")
+        else:
+            gain = keep.tile([P, MID_PASSES, BANK], BF16, name="gain")
+            shift = keep.tile([P, MID_PASSES, BANK], BF16, name="shift")
+
+        def sorted_row(first):
+            return vector_row[:, first : first + BANK]
 
         def spread_vectors():
-            for v, spread in enumerate((bias_f2, gain, shift)):
+            for g in range(MID_PASSES):
+                bank = ring.tile([P, BANK], F32, tag="ring")
+                nc.tensor.matmul(
+                    bank[:],
+                    lhsT=ones[:], rhs=sorted_row(g * BANK), start=True, stop=True,
+                )
+                nc.scalar.copy(out=bias_f2[:, g], in_=bank[:])
+            for v, spread in ((1, gain), (2, shift)):
                 for g in range(MID_PASSES):
-                    bank = ring.tile([P, BANK], F32, tag="ring")
-                    first = (MID_PASSES * v + g) * BANK
-                    nc.tensor.matmul(
-                        bank[:], lhsT=ones[:], rhs=vector_row[:, first : first + BANK], start=True, stop=True
-                    )
-                    nc.vector.tensor_copy(
-                        out=spread[:, g], in_=bank[:].rearrange("q (p t) -> q t p", t=PACK)
-                    )
+                    if PSUM_CONST:
+                        nc.tensor.matmul(
+                            spread[:, g],
+                            lhsT=ones[:], rhs=sorted_row((MID_PASSES * v + g) * BANK), start=True, stop=True,
+                        )
+                    else:
+                        bank = ring.tile([P, BANK], F32, tag="ring")
+                        nc.tensor.matmul(
+                            bank[:],
+                            lhsT=ones[:], rhs=sorted_row((MID_PASSES * v + g) * BANK), start=True, stop=True,
+                        )
+                        nc.scalar.copy(out=spread[:, g], in_=bank[:])
             bank = ring.tile([P, BANK], F32, tag="ring")
             nc.tensor.matmul(bank[:], lhsT=ones[:], rhs=vector_row[:, 3 * MID :], start=True, stop=True)
-            nc.vector.tensor_copy(out=bias_h[:], in_=bank[:])
+            nc.scalar.copy(out=bias_h[:], in_=bank[:])
 
         h_grouped = {}
         h_codes = {}
         h_planes = {}
-
         h_sorted = {}
 
         def h_words(j):
@@ -166,58 +198,65 @@ def tile_tsh_mid_block_pb_kernel(
                 )
             h_grouped[j] = grouped
 
-        def quantise_h(j):
-            codes = work.tile([P, FFN_PASSES * P], U32, align_bytes=64, tag="h_codes", bufs=3)
-            planes = work.tile([P, FFN_PASSES * P], U8, align_bytes=64, tag="h_planes", bufs=3)
-            for a in range(2):
+        def quantise_h(j, pieces=2):
+            codes = work.tile([P, FFN_PASSES * P], U32, align_bytes=64, tag="h_codes", bufs=4)
+            planes = work.tile([P, FFN_PASSES * P], U8, align_bytes=64, tag="h_planes", bufs=4)
+            w = FFN_PASSES * P // pieces
+            for a in range(pieces):
                 nc.vector.quantize_mx(
-                    out=codes[:, a * 512 : (a + 1) * 512].bitcast(FP8X4),
-                    scales=planes[:, a * 512 : (a + 1) * 512],
-                    in_=h_grouped[j][:, a * 2048 : (a + 1) * 2048],
+                    out=codes[:, a * w : (a + 1) * w].bitcast(FP8X4),
+                    scales=planes[:, a * w : (a + 1) * w],
+                    in_=h_grouped[j][:, a * w * PACK : (a + 1) * w * PACK],
                 )
             h_codes[j] = codes
             h_planes[j] = planes
 
         res1_biased = {}
 
-        def add_bias_to_residual(j):
-            biased = work.tile([P, MID_PASSES, PACK, P], F32, tag="res1_biased", bufs=3)
-            nc.vector.tensor_tensor(
-                out=biased[:],
-                in0=res1_sb[j][:].rearrange("q (g p t) -> q g t p", g=MID_PASSES, t=PACK),
-                in1=bias_f2[:],
-                op=ALU.add,
-            )
+        def add_bias_to_residual(j, engine):
+            biased = work.tile([P, MID_PASSES, BANK], F32, tag="res1_biased", bufs=3)
+            for g in range(MID_PASSES):
+                engine.tensor_tensor(
+                    out=biased[:, g],
+                    in0=res1_sb[j][:, g * BANK : (g + 1) * BANK],
+                    in1=bias_f2[:, g],
+                    op=ALU.add,
+                )
             res1_biased[j] = biased
 
         acc = {}
         res2 = {}
         row_sums = {}
 
-        def first_matmul(j, half):
-            bank = acc_pool.tile([P, BANK], F32, tag="acc")
+        def first_matmul(group, half, borrowed=False):
+            for j in group:
+                if borrowed:
+                    bank = ring.tile([P, BANK], F32, tag="ring")
+                else:
+                    bank = acc_pool.tile([P, BANK], F32, tag="acc")
+                acc[(j, half)] = bank
             for g in range(FFN_PASSES):
                 plane = PACK * (g % PLANES_PER_TILE)
-                nc.tensor.matmul_mx(
-                    out=bank[:],
-                    lhsT=h_codes[j][:, g * P : (g + 1) * P].bitcast(FP8X4),
-                    lhsT_scale=h_planes[j][:, g * P : (g + 1) * P],
-                    rhs=w_f2_sb[:, g, half * BANK : (half + 1) * BANK].bitcast(FP8X4),
-                    rhs_scale=w_f2_planes[plane:P, g // PLANES_PER_TILE, half * BANK : (half + 1) * BANK],
-                    start=(g == 0),
-                    stop=(g == FFN_PASSES - 1),
-                )
-            acc[(j, half)] = bank
+                for j in group:
+                    nc.tensor.matmul_mx(
+                        out=acc[(j, half)][:],
+                        lhsT=h_codes[j][:, g * P : (g + 1) * P].bitcast(FP8X4),
+                        lhsT_scale=h_planes[j][:, g * P : (g + 1) * P],
+                        rhs=w_f2_sb[:, g, half * BANK : (half + 1) * BANK].bitcast(FP8X4),
+                        rhs_scale=w_f2_planes[plane:P, g // PLANES_PER_TILE, half * BANK : (half + 1) * BANK],
+                        start=(g == 0),
+                        stop=(g == FFN_PASSES - 1),
+                    )
 
         def add_residual(j, half):
             if half == 0:
-                res2_tile = work.tile([P, MID_PASSES, PACK, P], F32, tag="res2")
+                res2_tile = work.tile([P, MID_PASSES, BANK], F32, tag="res2", bufs=3)
                 res2[j] = res2_tile
                 sums = work.tile([P, MID_PASSES], F32, tag="row_sums", bufs=3)
                 row_sums[j] = sums
             nc.vector.scalar_tensor_tensor(
                 out=res2[j][:, half],
-                in0=acc[(j, half)][:].rearrange("q (p t) -> q t p", t=PACK),
+                in0=acc[(j, half)][:],
                 scalar=1.0,
                 in1=res1_biased[j][:, half],
                 op0=ALU.mult,
@@ -248,7 +287,7 @@ def tile_tsh_mid_block_pb_kernel(
             sum_squares = work.tile([P, 1], F32, tag="sum_squares")
             nc.scalar.activation(
                 out=squares[:],
-                in_=res2[j][:].rearrange("q g t p -> q (g t p)"),
+                in_=res2[j][:].rearrange("q g n -> q (g n)"),
                 func=ACT.Square,
                 bias=minus_mean[j][:, 0:1],
                 scale=1.0,
@@ -261,28 +300,33 @@ def tile_tsh_mid_block_pb_kernel(
             rstd_input[j] = std
 
         def centre_and_gain(j):
-            gained = work.tile([P, MID_PASSES, PACK * P], F32, tag="gained")
-            for g in range(MID_PASSES):
-                nc.vector.scalar_tensor_tensor(
-                    out=gained[:, g],
-                    in0=res2[j][:, g].rearrange("q t p -> q (t p)"),
-                    scalar=minus_mean[j][:, 0:1],
-                    in1=gain[:, g].rearrange("q t p -> q (t p)"),
-                    op0=ALU.add,
-                    op1=ALU.mult,
-                )
+            gained = work.tile([P, MID], F32, tag="gained")
+            nc.vector.scalar_tensor_tensor(
+                out=gained[:],
+                in0=res2[j][:].rearrange("q g n -> q (g n)"),
+                scalar=minus_mean[j][:, 0:1],
+                in1=gain[:].rearrange("q g n -> q (g n)"),
+                op0=ALU.add,
+                op1=ALU.mult,
+            )
             gained_rows[j] = gained
 
-        def scale_and_shift(j):
+        rstds = {}
+
+        def reciprocal(j):
             rstd = work.tile([P, 1], F32, tag="rstd")
             nc.vector.reciprocal(out=rstd[:], in_=rstd_input[j][:])
-            normed = work.tile([P, MID_PASSES, PACK * P], BF16, tag="norm2", bufs=3)
-            for g in range(MID_PASSES):
+            rstds[j] = rstd
+
+        def scale_and_shift(j, pieces=1):
+            normed = work.tile([P, MID], BF16, tag="norm2", bufs=3)
+            w = MID // pieces
+            for a in range(pieces):
                 nc.vector.scalar_tensor_tensor(
-                    out=normed[:, g],
-                    in0=gained_rows[j][:, g],
-                    scalar=rstd[:, 0:1],
-                    in1=shift[:, g].rearrange("q t p -> q (t p)"),
+                    out=normed[:, a * w : (a + 1) * w],
+                    in0=gained_rows[j][:, a * w : (a + 1) * w],
+                    scalar=rstds[j][:, 0:1],
+                    in1=shift[:].rearrange("q g n -> q (g n)")[:, a * w : (a + 1) * w],
                     op0=ALU.mult,
                     op1=ALU.add,
                 )
@@ -293,24 +337,21 @@ def tile_tsh_mid_block_pb_kernel(
         norm2_planes = {}
 
         def transpose_norm2(j):
-            bank = ring.tile([P, MID_PASSES * PACK, P], BF16, tag="ring")
-            columns = norm2[j][:].rearrange("q g n -> q (g n)")
-            for gt in range(MID_PASSES * PACK):
-                nc.tensor.transpose(bank[:, gt, :], columns[:, gt * P : (gt + 1) * P], ident_bf16[:])
-            grouped = work.tile([P, MID_PASSES, P, PACK], BF16, align_bytes=64, tag="norm2_grouped")
-            by_pass = bank[:].rearrange("q (g t) c -> q g c t", g=MID_PASSES)
-            for g in range(MID_PASSES):
-                nc.scalar.copy(out=grouped[:, g], in_=by_pass[:, g])
+            bank = ring.tile([P, MID_PASSES, 2, P], F32, tag="ring")
+            words = norm2[j][:].bitcast(F32).rearrange("q (g p u) -> q g u p", g=MID_PASSES, u=2)
+            for gu in range(MID_PASSES * 2):
+                nc.tensor.transpose(bank[:, gu // 2, gu % 2, :], words[:, gu // 2, gu % 2, :], ident_f32[:])
+            grouped = work.tile([P, MID], BF16, align_bytes=64, tag="norm2_grouped")
+            nc.scalar.copy(
+                out=grouped[:].bitcast(F32).rearrange("q (g c u) -> q g c u", g=MID_PASSES, u=2),
+                in_=bank[:].rearrange("q g u c -> q g c u"),
+            )
             norm2_grouped[j] = grouped
 
         def quantise_norm2(j):
             codes = work.tile([P, MID_PASSES * P], U32, align_bytes=64, tag="norm2_codes")
             planes = work.tile([P, MID_PASSES * P], U8, align_bytes=64, tag="norm2_planes")
-            nc.vector.quantize_mx(
-                out=codes[:].bitcast(FP8X4),
-                scales=planes[:],
-                in_=norm2_grouped[j][:].rearrange("q g c t -> q (g c t)"),
-            )
+            nc.vector.quantize_mx(out=codes[:].bitcast(FP8X4), scales=planes[:], in_=norm2_grouped[j][:])
             norm2_codes[j] = codes
             norm2_planes[j] = planes
 
@@ -340,43 +381,75 @@ def tile_tsh_mid_block_pb_kernel(
         def tiles(r):
             return rounds[r] if 0 <= r < len(rounds) else ()
 
-        for j in tiles(0):
+        side = nc.gpsimd if GP_BIAS else nc.vector
+        for j in (0, 1):
             transpose_h(j)
             quantise_h(j)
         spread_vectors()
-        for j in tiles(0):
-            add_bias_to_residual(j)
-        for r in range(len(rounds) + 3):
+        first_matmul((0, 1), 0)
+        first_matmul((0, 1), 1, borrowed=True)
+        for j in (0, 1):
+            add_bias_to_residual(j, nc.vector)
+            add_residual(j, 0)
+        transpose_h(2)
+        for j in (0, 1):
+            add_residual(j, 1)
+            mean(j)
+            deviation(j)
+        add_bias_to_residual(2, side)
+        centre_and_gain(0)
+        quantise_h(2)
+        centre_and_gain(1)
+        transpose_h(3)
+        sort_h(4)
+        for j in (0, 1):
+            reciprocal(j)
+        for j in (0, 1):
+            scale_and_shift(j)
+        first_matmul((2,), 0)
+        quantise_h(3)
+        add_bias_to_residual(3, side)
+        add_residual(2, 0)
+        first_matmul((2,), 1)
+        for r in range(2, len(rounds) + 3):
             for j in tiles(r + 3):
                 load_h(j)
                 load_res1(j)
             for j in tiles(r - 1):
                 add_residual(j, 1)
                 mean(j)
-                deviation(j)
+            last = r == len(rounds)
+            if last:
+                for j in tiles(r - 1):
+                    deviation(j)
+            for j in tiles(r - 2):
+                transpose_norm2(j)
+            if not last:
+                for j in tiles(r - 1):
+                    deviation(j)
             for j in tiles(r - 3):
                 store(j)
             for j in tiles(r - 1):
                 centre_and_gain(j)
             for j in tiles(r + 1):
-                add_bias_to_residual(j)
-            for j in tiles(r - 1):
-                scale_and_shift(j)
-            for j in tiles(r - 2):
-                transpose_norm2(j)
+                add_bias_to_residual(j, side)
             for j in tiles(r + 1):
                 transpose_h(j)
             for j in tiles(r + 2):
-                if j >= FIRST_SORTED:
-                    sort_h(j)
-            for j in tiles(r):
-                first_matmul(j, 0)
-                add_residual(j, 0)
+                sort_h(j)
             for j in tiles(r - 2):
                 quantise_norm2(j)
-            for j in tiles(r + 1):
-                quantise_h(j)
+            for j in tiles(r - 1):
+                reciprocal(j)
             for j in tiles(r):
-                first_matmul(j, 1)
+                first_matmul((j,), 0)
+            for j in tiles(r - 1):
+                scale_and_shift(j, 2 if last else 1)
+            for j in tiles(r):
+                add_residual(j, 0)
+            for j in tiles(r + 1):
+                quantise_h(j, 1)
+            for j in tiles(r):
+                first_matmul((j,), 1)
             for j in tiles(r - 2):
                 second_matmul(j)

@@ -215,13 +215,12 @@ def tile_tsh_mid_block_pb_kernel(
 
         def add_bias_to_residual(j, engine):
             biased = work.tile([P, MID_PASSES, BANK], F32, tag="res1_biased", bufs=3)
-            for g in range(MID_PASSES):
-                engine.tensor_tensor(
-                    out=biased[:, g],
-                    in0=res1_sb[j][:, g * BANK : (g + 1) * BANK],
-                    in1=bias_f2[:, g],
-                    op=ALU.add,
-                )
+            engine.tensor_tensor(
+                out=biased[:].rearrange("q g n -> q (g n)"),
+                in0=res1_sb[j][:],
+                in1=bias_f2[:].rearrange("q g n -> q (g n)"),
+                op=ALU.add,
+            )
             res1_biased[j] = biased
 
         acc = {}
@@ -336,22 +335,32 @@ def tile_tsh_mid_block_pb_kernel(
         norm2_codes = {}
         norm2_planes = {}
 
-        def transpose_norm2(j):
+        def transpose_norm2(j, pieces=1):
             bank = ring.tile([P, MID_PASSES, 2, P], F32, tag="ring")
             words = norm2[j][:].bitcast(F32).rearrange("q (g p u) -> q g u p", g=MID_PASSES, u=2)
-            for gu in range(MID_PASSES * 2):
-                nc.tensor.transpose(bank[:, gu // 2, gu % 2, :], words[:, gu // 2, gu % 2, :], ident_f32[:])
             grouped = work.tile([P, MID], BF16, align_bytes=64, tag="norm2_grouped")
-            nc.scalar.copy(
-                out=grouped[:].bitcast(F32).rearrange("q (g c u) -> q g c u", g=MID_PASSES, u=2),
-                in_=bank[:].rearrange("q g u c -> q g c u"),
-            )
+            grouped_words = grouped[:].bitcast(F32).rearrange("q (g c u) -> q g c u", g=MID_PASSES, u=2)
+            n = MID_PASSES // pieces
+            for a in range(pieces):
+                for g in range(a * n, (a + 1) * n):
+                    for u in range(2):
+                        nc.tensor.transpose(bank[:, g, u, :], words[:, g, u, :], ident_f32[:])
+                nc.scalar.copy(
+                    out=grouped_words[:, a * n : (a + 1) * n],
+                    in_=bank[:, a * n : (a + 1) * n].rearrange("q g u c -> q g c u"),
+                )
             norm2_grouped[j] = grouped
 
-        def quantise_norm2(j):
+        def quantise_norm2(j, pieces=1):
             codes = work.tile([P, MID_PASSES * P], U32, align_bytes=64, tag="norm2_codes")
             planes = work.tile([P, MID_PASSES * P], U8, align_bytes=64, tag="norm2_planes")
-            nc.vector.quantize_mx(out=codes[:].bitcast(FP8X4), scales=planes[:], in_=norm2_grouped[j][:])
+            w = MID_PASSES * P // pieces
+            for a in range(pieces):
+                nc.vector.quantize_mx(
+                    out=codes[:, a * w : (a + 1) * w].bitcast(FP8X4),
+                    scales=planes[:, a * w : (a + 1) * w],
+                    in_=norm2_grouped[j][:, a * w * PACK : (a + 1) * w * PACK],
+                )
             norm2_codes[j] = codes
             norm2_planes[j] = planes
 
@@ -372,7 +381,7 @@ def tile_tsh_mid_block_pb_kernel(
             product[j] = bank
 
         def store(j):
-            result = work.tile([P, D_OUT], F32, tag="result", bufs=3)
+            result = work.tile([P, D_OUT], F32, tag="result", bufs=4)
             nc.vector.tensor_tensor(out=result[:], in0=product[j][:], in1=bias_h[:], op=ALU.add)
             nc.sync.dma_start(out=out_rows[j * P : (j + 1) * P, :], in_=result[:])
 
@@ -396,7 +405,6 @@ def tile_tsh_mid_block_pb_kernel(
             add_residual(j, 1)
             mean(j)
             deviation(j)
-        add_bias_to_residual(2, side)
         centre_and_gain(0)
         quantise_h(2)
         centre_and_gain(1)
@@ -404,47 +412,43 @@ def tile_tsh_mid_block_pb_kernel(
         sort_h(4)
         for j in (0, 1):
             reciprocal(j)
-        for j in (0, 1):
             scale_and_shift(j)
+        add_bias_to_residual(2, side)
         first_matmul((2,), 0)
         quantise_h(3)
-        add_bias_to_residual(3, side)
         add_residual(2, 0)
+        add_bias_to_residual(3, side)
         first_matmul((2,), 1)
-        for r in range(2, len(rounds) + 3):
+        for r in range(2, len(rounds)):
             for j in tiles(r + 3):
                 load_h(j)
                 load_res1(j)
             for j in tiles(r - 1):
                 add_residual(j, 1)
-                mean(j)
-            last = r == len(rounds)
-            if last:
-                for j in tiles(r - 1):
-                    deviation(j)
-            for j in tiles(r - 2):
-                transpose_norm2(j)
-            if not last:
-                for j in tiles(r - 1):
-                    deviation(j)
             for j in tiles(r - 3):
                 store(j)
             for j in tiles(r - 1):
-                centre_and_gain(j)
+                mean(j)
+            for j in tiles(r - 2):
+                transpose_norm2(j)
+            for j in tiles(r - 1):
+                deviation(j)
             for j in tiles(r + 1):
                 add_bias_to_residual(j, side)
+            for j in tiles(r - 1):
+                centre_and_gain(j)
             for j in tiles(r + 1):
                 transpose_h(j)
             for j in tiles(r + 2):
                 sort_h(j)
-            for j in tiles(r - 2):
-                quantise_norm2(j)
             for j in tiles(r - 1):
                 reciprocal(j)
+            for j in tiles(r - 2):
+                quantise_norm2(j)
             for j in tiles(r):
                 first_matmul((j,), 0)
             for j in tiles(r - 1):
-                scale_and_shift(j, 2 if last else 1)
+                scale_and_shift(j)
             for j in tiles(r):
                 add_residual(j, 0)
             for j in tiles(r + 1):
@@ -453,3 +457,18 @@ def tile_tsh_mid_block_pb_kernel(
                 first_matmul((j,), 1)
             for j in tiles(r - 2):
                 second_matmul(j)
+        add_residual(7, 1)
+        mean(7)
+        deviation(7)
+        centre_and_gain(7)
+        transpose_norm2(6)
+        reciprocal(7)
+        scale_and_shift(7, 2)
+        transpose_norm2(7, 2)
+        quantise_norm2(6)
+        store(5)
+        second_matmul(6)
+        quantise_norm2(7, 2)
+        second_matmul(7)
+        store(6)
+        store(7)

@@ -63,13 +63,9 @@ def tile_tsh_mid_block_pb_kernel(
         ident_f32 = keep.tile([P, P], F32)
         make_identity(nc, ident_f32[:])
 
-        for v, vector in enumerate((b_f2, g2, be2)):
-            nc.scalar.dma_start(out=vector_row[0:1, v * MID : (v + 1) * MID], in_=vector.unsqueeze(0))
-        nc.scalar.dma_start(out=vector_row[0:1, 3 * MID :], in_=b_h.unsqueeze(0))
-
         h_sb = {}
         res1_sb = {}
-        w_f2_sb = keep.tile([P, FFN_PASSES, MID], U32, align_bytes=64)
+        w_f2_sb = keep.tile([P, MID_PASSES, FFN_PASSES, BANK], U32, align_bytes=64)
         w_h_sb = keep.tile([P, MID_PASSES, D_OUT], U32, align_bytes=64)
 
         def load_h(j, pieces=1):
@@ -87,14 +83,27 @@ def tile_tsh_mid_block_pb_kernel(
             nc.sync.dma_start(out=res1_tile[:], in_=res1_rows[j * P : (j + 1) * P, :])
             res1_sb[j] = res1_tile
 
-        def load_w_f2(half):
-            for g in range(FFN_PASSES):
+        def load_w_f2(half, first, count):
+            nc.sync.dma_start(
+                out=w_f2_sb[:, half, first : first + count, :].bitcast(I32),
+                in_=w_f2_words[first : first + count]
+                .rearrange("g p n t -> p g (n t)")[:, :, half * BANK * PACK : (half + 1) * BANK * PACK]
+                .bitcast(I32),
+            )
+
+        def load_w_f2_scales(a):
+            for quadrant in range(4):
                 nc.sync.dma_start(
-                    out=w_f2_sb[:, g, half * BANK : (half + 1) * BANK].bitcast(I32),
-                    in_=w_f2_words[g]
-                    .rearrange("p n t -> p (n t)")[:, half * BANK * PACK : (half + 1) * BANK * PACK]
-                    .bitcast(I32),
+                    out=w_f2_planes[32 * quadrant : 32 * quadrant + 16, a, :].bitcast(I32),
+                    in_=w_f2_scales[
+                        PLANES_PER_TILE * a : PLANES_PER_TILE * (a + 1), 4 * quadrant : 4 * quadrant + 4, :
+                    ].bitcast(I32),
                 )
+
+        def load_vectors():
+            for v, vector in enumerate((b_f2, g2, be2)):
+                nc.sync.dma_start(out=vector_row[0:1, v * MID : (v + 1) * MID], in_=vector.unsqueeze(0))
+            nc.sync.dma_start(out=vector_row[0:1, 3 * MID :], in_=b_h.unsqueeze(0))
 
         def load_w_h():
             nc.sync.dma_start(
@@ -106,22 +115,21 @@ def tile_tsh_mid_block_pb_kernel(
                     in_=w_h_scales[:, 4 * quadrant : 4 * quadrant + 4, :].bitcast(I32),
                 )
 
-        for j in range(2):
-            load_h(j, 4)
-        for a in range(FFN_PASSES // PLANES_PER_TILE):
-            for quadrant in range(4):
-                nc.sync.dma_start(
-                    out=w_f2_planes[32 * quadrant : 32 * quadrant + 16, a, :].bitcast(I32),
-                    in_=w_f2_scales[
-                        PLANES_PER_TILE * a : PLANES_PER_TILE * (a + 1), 4 * quadrant : 4 * quadrant + 4, :
-                    ].bitcast(I32),
-                )
-        load_w_f2(0)
+        load_h(0, 2)
+        load_w_f2_scales(0)
+        load_h(1, 2)
+        load_w_f2(0, 0, 2)
+        load_w_f2_scales(1)
+        load_w_f2(0, 2, 2)
+        load_w_f2(0, 4, 2)
+        load_w_f2(0, 6, 2)
+        load_vectors()
         for j in range(2):
             load_res1(j)
-        load_w_f2(1)
+        for g in range(0, 8, 2):
+            load_w_f2(1, g, 2)
         for j in range(2, 4):
-            load_h(j, 4)
+            load_h(j, 2)
         load_res1(2)
         load_h(4)
         load_w_h()
@@ -241,7 +249,7 @@ def tile_tsh_mid_block_pb_kernel(
                         out=acc[(j, half)][:],
                         lhsT=h_codes[j][:, g * P : (g + 1) * P].bitcast(FP8X4),
                         lhsT_scale=h_planes[j][:, g * P : (g + 1) * P],
-                        rhs=w_f2_sb[:, g, half * BANK : (half + 1) * BANK].bitcast(FP8X4),
+                        rhs=w_f2_sb[:, half, g, :].bitcast(FP8X4),
                         rhs_scale=w_f2_planes[plane:P, g // PLANES_PER_TILE, half * BANK : (half + 1) * BANK],
                         start=(g == 0),
                         stop=(g == FFN_PASSES - 1),
@@ -394,8 +402,8 @@ def tile_tsh_mid_block_pb_kernel(
         for j in (0, 1):
             transpose_h(j)
             quantise_h(j)
-        spread_vectors()
         first_matmul((0, 1), 0)
+        spread_vectors()
         first_matmul((0, 1), 1, borrowed=True)
         for j in (0, 1):
             add_bias_to_residual(j, nc.vector)

@@ -50,13 +50,13 @@ def tile_tsh_mid_block_pb_kernel(
         ring = ctx.enter_context(tc.psum_pool(name="ring", bufs=4 if PSUM_CONST else 6))
         fixed = ctx.enter_context(tc.psum_pool(name="fixed", bufs=1)) if PSUM_CONST else None
 
-        w_f2_planes = keep.tile([P, FFN_PASSES // PLANES_PER_TILE, MID], U8, align_bytes=64)
+        w_f2_planes = keep.tile([P, FFN_PASSES // PLANES_PER_TILE, MID], U8, align_bytes=256)
         nc.vector.memset(w_f2_planes[:].rearrange("q a n -> q (a n)").bitcast(I32), 0)
         vector_row = keep.tile([P, 3 * MID + D_OUT], BF16)
         nc.vector.memset(vector_row[:].bitcast(I32), 0)
         ones = keep.tile([P, P], BF16)
         nc.vector.memset(ones[:], 1.0)
-        w_h_planes = keep.tile([P, D_OUT], U8, align_bytes=64)
+        w_h_planes = keep.tile([P, D_OUT], U8, align_bytes=256)
         nc.vector.memset(w_h_planes[:].bitcast(I32), 0)
         eps = keep.tile([P, 1], F32)
         nc.vector.memset(eps[:], LN_EPS)
@@ -65,8 +65,8 @@ def tile_tsh_mid_block_pb_kernel(
 
         h_sb = {}
         res1_sb = {}
-        w_f2_sb = keep.tile([P, MID_PASSES, FFN_PASSES, BANK], U32, align_bytes=64)
-        w_h_sb = keep.tile([P, MID_PASSES, D_OUT], U32, align_bytes=64)
+        w_f2_sb = keep.tile([P, MID_PASSES, FFN_PASSES, BANK], U32, align_bytes=256)
+        w_h_sb = keep.tile([P, MID_PASSES, D_OUT], U32, align_bytes=256)
 
         def load_h(j, pieces=1):
             h_tile = h_pool.tile([P, FFN], BF16, tag="h")
@@ -193,7 +193,7 @@ def tile_tsh_mid_block_pb_kernel(
 
         def transpose_h(j):
             words = h_sorted[j][:] if j in h_sorted else h_words(j)
-            grouped = work.tile([P, FFN], BF16, align_bytes=64, tag="h_grouped")
+            grouped = work.tile([P, FFN], BF16, align_bytes=256, tag="h_grouped")
             grouped_words = grouped[:].bitcast(F32).rearrange("q (g c u) -> q g c u", g=FFN_PASSES, u=2)
             for b in range(FFN_PASSES // 2):
                 bank = ring.tile([P, 2, 2, P], F32, tag="ring")
@@ -207,8 +207,8 @@ def tile_tsh_mid_block_pb_kernel(
             h_grouped[j] = grouped
 
         def quantise_h(j, pieces=2):
-            codes = work.tile([P, FFN_PASSES * P], U32, align_bytes=64, tag="h_codes", bufs=4)
-            planes = work.tile([P, FFN_PASSES * P], U8, align_bytes=64, tag="h_planes", bufs=4)
+            codes = work.tile([P, FFN_PASSES * P], U32, align_bytes=256, tag="h_codes", bufs=4)
+            planes = work.tile([P, FFN_PASSES * P], U8, align_bytes=256, tag="h_planes", bufs=4)
             w = FFN_PASSES * P // pieces
             for a in range(pieces):
                 nc.vector.quantize_mx(
@@ -346,7 +346,7 @@ def tile_tsh_mid_block_pb_kernel(
         def transpose_norm2(j, pieces=1):
             bank = ring.tile([P, MID_PASSES, 2, P], F32, tag="ring")
             words = norm2[j][:].bitcast(F32).rearrange("q (g p u) -> q g u p", g=MID_PASSES, u=2)
-            grouped = work.tile([P, MID], BF16, align_bytes=64, tag="norm2_grouped")
+            grouped = work.tile([P, MID], BF16, align_bytes=256, tag="norm2_grouped")
             grouped_words = grouped[:].bitcast(F32).rearrange("q (g c u) -> q g c u", g=MID_PASSES, u=2)
             n = MID_PASSES // pieces
             for a in range(pieces):
@@ -360,8 +360,8 @@ def tile_tsh_mid_block_pb_kernel(
             norm2_grouped[j] = grouped
 
         def quantise_norm2(j, pieces=1):
-            codes = work.tile([P, MID_PASSES * P], U32, align_bytes=64, tag="norm2_codes")
-            planes = work.tile([P, MID_PASSES * P], U8, align_bytes=64, tag="norm2_planes")
+            codes = work.tile([P, MID_PASSES * P], U32, align_bytes=256, tag="norm2_codes")
+            planes = work.tile([P, MID_PASSES * P], U8, align_bytes=256, tag="norm2_planes")
             w = MID_PASSES * P // pieces
             for a in range(pieces):
                 nc.vector.quantize_mx(

@@ -286,7 +286,7 @@ def tile_tsh_mid_block_pb_kernel(
             )
             minus_mean[j] = negative
 
-        rstd_input = {}
+        rstds = {}
         gained_rows = {}
 
         def deviation(j):
@@ -300,11 +300,11 @@ def tile_tsh_mid_block_pb_kernel(
                 scale=1.0,
                 accum_out=sum_squares[:, 0:1],
             )
-            std = work.tile([P, 1], F32, tag="std")
+            rstd = work.tile([P, 1], F32, tag="rstd", bufs=3)
             nc.scalar.activation(
-                out=std[:], in_=sum_squares[:], func=ACT.Sqrt, bias=eps[:, 0:1], scale=1.0 / MID
+                out=rstd[:], in_=sum_squares[:], func=ACT.Abs_reciprocal_sqrt, bias=eps[:, 0:1], scale=1.0 / MID
             )
-            rstd_input[j] = std
+            rstds[j] = rstd
 
         def centre_and_gain(j):
             gained = work.tile([P, MID], F32, tag="gained")
@@ -318,12 +318,8 @@ def tile_tsh_mid_block_pb_kernel(
             )
             gained_rows[j] = gained
 
-        rstds = {}
-
         def reciprocal(j):
-            rstd = work.tile([P, 1], F32, tag="rstd")
-            nc.vector.reciprocal(out=rstd[:], in_=rstd_input[j][:])
-            rstds[j] = rstd
+            return None
 
         def scale_and_shift(j, pieces=1):
             normed = work.tile([P, MID], BF16, tag="norm2", bufs=3)

@@ -100,10 +100,8 @@ def tile_tsh_mid_block_pb_kernel(
                     ].bitcast(I32),
                 )
 
-        def load_vectors():
-            for v, vector in enumerate((b_f2, g2, be2)):
-                nc.sync.dma_start(out=vector_row[0:1, v * MID : (v + 1) * MID], in_=vector.unsqueeze(0))
-            nc.sync.dma_start(out=vector_row[0:1, 3 * MID :], in_=b_h.unsqueeze(0))
+        def load_vector(v, vector):
+            nc.sync.dma_start(out=vector_row[0:1, v * MID : v * MID + vector.shape[0]], in_=vector.unsqueeze(0))
 
         def load_w_h():
             nc.sync.dma_start(
@@ -118,12 +116,15 @@ def tile_tsh_mid_block_pb_kernel(
         load_h(0, 2)
         load_w_f2_scales(0)
         load_h(1, 2)
+        load_vector(0, b_f2)
+        load_vector(1, g2)
+        load_vector(2, be2)
+        load_vector(3, b_h)
         load_w_f2(0, 0, 2)
         load_w_f2_scales(1)
         load_w_f2(0, 2, 2)
         load_w_f2(0, 4, 2)
         load_w_f2(0, 6, 2)
-        load_vectors()
         for j in range(2):
             load_res1(j)
         for g in range(0, 8, 2):
@@ -150,31 +151,25 @@ def tile_tsh_mid_block_pb_kernel(
         def sorted_row(first):
             return vector_row[:, first : first + BANK]
 
-        def spread_vectors():
-            for g in range(MID_PASSES):
-                bank = ring.tile([P, BANK], F32, tag="ring")
-                nc.tensor.matmul(
-                    bank[:],
-                    lhsT=ones[:], rhs=sorted_row(g * BANK), start=True, stop=True,
-                )
-                nc.scalar.copy(out=bias_f2[:, g], in_=bank[:])
-            for v, spread in ((1, gain), (2, shift)):
-                for g in range(MID_PASSES):
-                    if PSUM_CONST:
-                        nc.tensor.matmul(
-                            spread[:, g],
-                            lhsT=ones[:], rhs=sorted_row((MID_PASSES * v + g) * BANK), start=True, stop=True,
-                        )
-                    else:
-                        bank = ring.tile([P, BANK], F32, tag="ring")
-                        nc.tensor.matmul(
-                            bank[:],
-                            lhsT=ones[:], rhs=sorted_row((MID_PASSES * v + g) * BANK), start=True, stop=True,
-                        )
-                        nc.scalar.copy(out=spread[:, g], in_=bank[:])
+        def spread_vector(first, spread):
             bank = ring.tile([P, BANK], F32, tag="ring")
-            nc.tensor.matmul(bank[:], lhsT=ones[:], rhs=vector_row[:, 3 * MID :], start=True, stop=True)
-            nc.scalar.copy(out=bias_h[:], in_=bank[:])
+            nc.tensor.matmul(bank[:], lhsT=ones[:], rhs=vector_row[:, first : first + BANK], start=True, stop=True)
+            nc.scalar.copy(out=spread, in_=bank[:])
+
+        def spread_b_f2():
+            for g in range(MID_PASSES):
+                spread_vector(g * BANK, bias_f2[:, g])
+
+        def spread_g2():
+            for g in range(MID_PASSES):
+                spread_vector(MID + g * BANK, gain[:, g])
+
+        def spread_be2():
+            for g in range(MID_PASSES):
+                spread_vector(2 * MID + g * BANK, shift[:, g])
+
+        def spread_b_h():
+            spread_vector(3 * MID, bias_h[:])
 
         h_grouped = {}
         h_codes = {}
@@ -306,6 +301,59 @@ def tile_tsh_mid_block_pb_kernel(
             )
             rstds[j] = rstd
 
+        shifts = {}
+        half_squares = {}
+
+        def shift_of_half(j):
+            shift_tile = work.tile([P, 2], F32, tag="half_shift", bufs=1)
+            for column, sign in ((0, -1.0), (1, 1.0)):
+                nc.scalar.activation(
+                    out=shift_tile[:, column : column + 1],
+                    in_=row_sums[j][:, 0:1],
+                    func=ACT.Copy,
+                    scale=sign / BANK,
+                )
+            shifts[j] = shift_tile
+
+        def squares_of_half(j, half):
+            squares = work.tile([P, MID], BF16, tag="squares")
+            total = work.tile([P, 1], F32, tag="half_squares", bufs=2)
+            nc.scalar.activation(
+                out=squares[:, :BANK],
+                in_=res2[j][:, half],
+                func=ACT.Square,
+                bias=shifts[j][:, 0:1],
+                scale=1.0,
+                accum_out=total[:, 0:1],
+            )
+            half_squares[(j, half)] = total
+
+        def deviation_from_halves(j):
+            offset = work.tile([P, 1], F32, tag="mean_offset", bufs=1)
+            nc.scalar.activation(out=offset[:], in_=minus_mean[j][:], func=ACT.Square, bias=shifts[j][:, 1:2], scale=1.0)
+            rest = work.tile([P, 1], F32, tag="variance_rest", bufs=1)
+            nc.scalar.activation(
+                out=rest[:], in_=offset[:], func=ACT.Identity, bias=first_half[j][:, 0:1], scale=-1.0
+            )
+            rstd = work.tile([P, 1], F32, tag="rstd", bufs=3)
+            nc.scalar.activation(
+                out=rstd[:],
+                in_=half_squares[(j, 1)][:],
+                func=ACT.Abs_reciprocal_sqrt,
+                bias=rest[:, 0:1],
+                scale=1.0 / MID,
+            )
+            rstds[j] = rstd
+
+        first_half = {}
+
+        def variance_of_first_half(j):
+            part = work.tile([P, 1], F32, tag="first_half", bufs=1)
+            nc.scalar.activation(
+                out=part[:], in_=half_squares[(j, 0)][:], func=ACT.Identity, bias=eps[:, 0:1], scale=1.0 / MID
+            )
+            first_half[j] = part
+
         def centre_and_gain(j):
             gained = work.tile([P, MID], F32, tag="gained")
             nc.vector.scalar_tensor_tensor(
@@ -340,18 +388,18 @@ def tile_tsh_mid_block_pb_kernel(
         norm2_planes = {}
 
         def transpose_norm2(j, pieces=1):
-            bank = ring.tile([P, MID_PASSES, 2, P], F32, tag="ring")
             words = norm2[j][:].bitcast(F32).rearrange("q (g p u) -> q g u p", g=MID_PASSES, u=2)
             grouped = work.tile([P, MID], BF16, align_bytes=256, tag="norm2_grouped")
             grouped_words = grouped[:].bitcast(F32).rearrange("q (g c u) -> q g c u", g=MID_PASSES, u=2)
             n = MID_PASSES // pieces
             for a in range(pieces):
-                for g in range(a * n, (a + 1) * n):
+                bank = ring.tile([P, n, 2, P], F32, tag="ring")
+                for g in range(n):
                     for u in range(2):
-                        nc.tensor.transpose(bank[:, g, u, :], words[:, g, u, :], ident_f32[:])
+                        nc.tensor.transpose(bank[:, g, u, :], words[:, a * n + g, u, :], ident_f32[:])
                 nc.scalar.copy(
                     out=grouped_words[:, a * n : (a + 1) * n],
-                    in_=bank[:, a * n : (a + 1) * n].rearrange("q g u c -> q g c u"),
+                    in_=bank[:].rearrange("q g u c -> q g c u"),
                 )
             norm2_grouped[j] = grouped
 
@@ -389,6 +437,7 @@ def tile_tsh_mid_block_pb_kernel(
             nc.vector.tensor_tensor(out=result[:], in0=product[j][:], in1=bias_h[:], op=ALU.add)
             nc.sync.dma_start(out=out_rows[j * P : (j + 1) * P, :], in_=result[:])
 
+        last = N_TILES - 1
         rounds = [(0, 1)] + [(j,) for j in range(2, N_TILES)]
 
         def tiles(r):
@@ -398,11 +447,15 @@ def tile_tsh_mid_block_pb_kernel(
         for j in (0, 1):
             transpose_h(j)
             quantise_h(j)
+        spread_b_f2()
+        spread_g2()
         first_matmul((0, 1), 0)
-        spread_vectors()
+        spread_be2()
+        spread_b_h()
         first_matmul((0, 1), 1, borrowed=True)
         for j in (0, 1):
             add_bias_to_residual(j, nc.vector)
+        for j in (0, 1):
             add_residual(j, 0)
         transpose_h(2)
         for j in (0, 1):
@@ -445,34 +498,38 @@ def tile_tsh_mid_block_pb_kernel(
                 transpose_h(j)
             for j in tiles(r + 2):
                 sort_h(j)
-            for j in tiles(r - 1):
-                reciprocal(j)
-            for j in tiles(r - 2):
-                quantise_norm2(j)
             for j in tiles(r):
                 first_matmul((j,), 0)
+            if r == len(rounds) - 1:
+                add_residual(last, 0)
+                shift_of_half(last)
+                squares_of_half(last, 0)
+                variance_of_first_half(last)
+            for j in tiles(r - 2):
+                quantise_norm2(j)
             for j in tiles(r - 1):
                 scale_and_shift(j)
-            for j in tiles(r):
-                add_residual(j, 0)
+            if r < len(rounds) - 1:
+                for j in tiles(r):
+                    add_residual(j, 0)
             for j in tiles(r + 1):
                 quantise_h(j, 1)
             for j in tiles(r):
                 first_matmul((j,), 1)
             for j in tiles(r - 2):
                 second_matmul(j)
-        add_residual(7, 1)
-        mean(7)
-        deviation(7)
-        centre_and_gain(7)
-        transpose_norm2(6)
-        reciprocal(7)
-        scale_and_shift(7, 2)
-        transpose_norm2(7, 2)
-        quantise_norm2(6)
-        store(5)
-        second_matmul(6)
-        quantise_norm2(7, 2)
-        second_matmul(7)
-        store(6)
-        store(7)
+        add_residual(last, 1)
+        mean(last)
+        squares_of_half(last, 1)
+        deviation_from_halves(last)
+        transpose_norm2(last - 1)
+        centre_and_gain(last)
+        scale_and_shift(last, 2)
+        quantise_norm2(last - 1)
+        transpose_norm2(last, 2)
+        store(last - 2)
+        second_matmul(last - 1)
+        quantise_norm2(last, 2)
+        second_matmul(last)
+        store(last - 1)
+        store(last)

@@ -63,6 +63,10 @@ def tile_tsh_mid_block_pb_kernel(
         ident_f32 = keep.tile([P, P], F32)
         make_identity(nc, ident_f32[:])
 
+        bias_f2 = keep.tile([P, MID_PASSES, BANK], BF16)
+        bias_h = keep.tile([P, D_OUT], BF16)
+        gain = keep.tile([P, MID_PASSES, BANK], BF16)
+        shift = keep.tile([P, MID_PASSES, BANK], BF16)
         h_sb = {}
         res1_sb = {}
         w_f2_sb = keep.tile([P, MID_PASSES, FFN_PASSES, BANK], U32, align_bytes=256)
@@ -101,7 +105,7 @@ def tile_tsh_mid_block_pb_kernel(
                 )
 
         def load_vector(v, vector):
-            nc.sync.dma_start(out=vector_row[0:1, v * MID : v * MID + vector.shape[0]], in_=vector.unsqueeze(0))
+            nc.gpsimd.dma_start(out=vector_row[0:1, v * MID : v * MID + vector.shape[0]], in_=vector.unsqueeze(0))
 
         def load_w_h():
             nc.sync.dma_start(
@@ -113,43 +117,34 @@ def tile_tsh_mid_block_pb_kernel(
                     in_=w_h_scales[:, 4 * quadrant : 4 * quadrant + 4, :].bitcast(I32),
                 )
 
+        load_vector(0, b_f2)
+        load_vector(1, g2)
         load_h(0, 2)
         load_w_f2_scales(0)
         load_h(1, 2)
-        load_vector(0, b_f2)
-        load_vector(1, g2)
-        load_vector(2, be2)
-        load_vector(3, b_h)
         load_w_f2(0, 0, 2)
         load_w_f2_scales(1)
         load_w_f2(0, 2, 2)
         load_w_f2(0, 4, 2)
         load_w_f2(0, 6, 2)
-        for j in range(2):
-            load_res1(j)
-        for g in range(0, 8, 2):
-            load_w_f2(1, g, 2)
-        for j in range(2, 4):
-            load_h(j, 2)
+        load_res1(0)
+        load_res1(1)
+        load_w_f2(1, 0, 2)
+        load_w_f2(1, 2, 2)
+        load_w_f2(1, 4, 2)
+        load_w_f2(1, 6, 2)
+        load_h(2, 2)
+        load_h(3, 2)
+        nc.sync.dma_start(out=shift[:].rearrange("q g n -> q (g n)"), in_=be2.partition_broadcast(P))
         load_res1(2)
         load_h(4)
         load_w_h()
+        nc.sync.dma_start(out=bias_h[:], in_=b_h.partition_broadcast(P))
         load_res1(3)
         load_res1(4)
         load_h(5)
         load_res1(5)
 
-        bias_f2 = keep.tile([P, MID_PASSES, BANK], BF16)
-        bias_h = keep.tile([P, D_OUT], BF16)
-        if PSUM_CONST:
-            gain = fixed.tile([P, MID_PASSES, BANK], BF16, name="gain")
-            shift = fixed.tile([P, MID_PASSES, BANK], BF16, name="shift")
-        else:
-            gain = keep.tile([P, MID_PASSES, BANK], BF16, name="gain")
-            shift = keep.tile([P, MID_PASSES, BANK], BF16, name="shift")
-
-        def sorted_row(first):
-            return vector_row[:, first : first + BANK]
 
         def spread_vector(first, spread):
             bank = ring.tile([P, BANK], F32, tag="ring")
@@ -448,10 +443,8 @@ def tile_tsh_mid_block_pb_kernel(
             transpose_h(j)
             quantise_h(j)
         spread_b_f2()
-        spread_g2()
         first_matmul((0, 1), 0)
-        spread_be2()
-        spread_b_h()
+        spread_g2()
         first_matmul((0, 1), 1, borrowed=True)
         for j in (0, 1):
             add_bias_to_residual(j, nc.vector)

@@ -133,10 +133,10 @@ def tile_tsh_mid_block_pb_kernel(
         load_w_f2(1, 2, 2)
         load_w_f2(1, 4, 2)
         load_w_f2(1, 6, 2)
+        load_res1(2)
         load_h(2, 2)
         load_h(3, 2)
         nc.sync.dma_start(out=shift[:].rearrange("q g n -> q (g n)"), in_=be2.partition_broadcast(P))
-        load_res1(2)
         load_h(4)
         load_w_h()
         nc.sync.dma_start(out=bias_h[:], in_=b_h.partition_broadcast(P))
@@ -262,7 +262,7 @@ def tile_tsh_mid_block_pb_kernel(
             )
 
         minus_mean = {}
-        norm2 = {}
+        norm2_words = {}
 
         def mean(j):
             negative = work.tile([P, 1], F32, tag="minus_mean", bufs=3)
@@ -366,24 +366,37 @@ def tile_tsh_mid_block_pb_kernel(
 
         def scale_and_shift(j, pieces=1):
             normed = work.tile([P, MID], BF16, tag="norm2", bufs=3)
-            w = MID // pieces
-            for a in range(pieces):
-                nc.vector.scalar_tensor_tensor(
-                    out=normed[:, a * w : (a + 1) * w],
-                    in0=gained_rows[j][:, a * w : (a + 1) * w],
-                    scalar=rstds[j][:, 0:1],
-                    in1=shift[:].rearrange("q g n -> q (g n)")[:, a * w : (a + 1) * w],
-                    op0=ALU.mult,
-                    op1=ALU.add,
-                )
-            norm2[j] = normed
+            if j == N_TILES - 1:
+                for g in range(MID_PASSES):
+                    nc.vector.scalar_tensor_tensor(
+                        out=normed[:, g * BANK : (g + 1) * BANK],
+                        in0=gained_rows[j][:, g * BANK : (g + 1) * BANK],
+                        scalar=rstds[j][:, 0:1],
+                        in1=shift[:, g],
+                        op0=ALU.mult,
+                        op1=ALU.add,
+                    )
+                norm2_words[j] = normed[:].bitcast(F32).rearrange("q (g p u) -> q g u p", g=MID_PASSES, u=2)
+            else:
+                pairs = "q (x u e) -> q u x e"
+                shift_pairs = shift[:].rearrange("q g n -> q (g n)").rearrange(pairs, u=2, e=2)
+                for u in range(2):
+                    nc.vector.scalar_tensor_tensor(
+                        out=normed[:, u * BANK : (u + 1) * BANK].rearrange("q (x e) -> q x e", e=2),
+                        in0=gained_rows[j][:].rearrange(pairs, u=2, e=2)[:, u],
+                        scalar=rstds[j][:, 0:1],
+                        in1=shift_pairs[:, u],
+                        op0=ALU.mult,
+                        op1=ALU.add,
+                    )
+                norm2_words[j] = normed[:].bitcast(F32).rearrange("q (u g p) -> q g u p", g=MID_PASSES, u=2)
 
         norm2_grouped = {}
         norm2_codes = {}
         norm2_planes = {}
 
         def transpose_norm2(j, pieces=1):
-            words = norm2[j][:].bitcast(F32).rearrange("q (g p u) -> q g u p", g=MID_PASSES, u=2)
+            words = norm2_words[j]
             grouped = work.tile([P, MID], BF16, align_bytes=256, tag="norm2_grouped")
             grouped_words = grouped[:].bitcast(F32).rearrange("q (g c u) -> q g c u", g=MID_PASSES, u=2)
             n = MID_PASSES // pieces
@@ -432,6 +445,34 @@ def tile_tsh_mid_block_pb_kernel(
             nc.vector.tensor_tensor(out=result[:], in0=product[j][:], in1=bias_h[:], op=ALU.add)
             nc.sync.dma_start(out=out_rows[j * P : (j + 1) * P, :], in_=result[:])
 
+        product_halves = []
+
+        def second_matmul_in_halves(j):
+            n = D_OUT // 2
+            for c in range(2):
+                bank = ring.tile([P, n], F32, tag="ring")
+                product_halves.append(bank)
+            for g in range(MID_PASSES):
+                for c in range(2):
+                    nc.tensor.matmul_mx(
+                        out=product_halves[c][:],
+                        lhsT=norm2_codes[j][:, g * P : (g + 1) * P].bitcast(FP8X4),
+                        lhsT_scale=norm2_planes[j][:, g * P : (g + 1) * P],
+                        rhs=w_h_sb[:, g, c * n : (c + 1) * n].bitcast(FP8X4),
+                        rhs_scale=w_h_planes[PACK * g : P, c * n : (c + 1) * n],
+                        start=(g == 0),
+                        stop=(g == MID_PASSES - 1),
+                    )
+
+        def store_halves(j):
+            n = D_OUT // 2
+            for c in range(2):
+                result = work.tile([P, n], F32, tag="result_half", bufs=2)
+                nc.vector.tensor_tensor(
+                    out=result[:], in0=product_halves[c][:], in1=bias_h[:, c * n : (c + 1) * n], op=ALU.add
+                )
+                nc.sync.dma_start(out=out_rows[j * P : (j + 1) * P, c * n : (c + 1) * n], in_=result[:])
+
         last = N_TILES - 1
         rounds = [(0, 1)] + [(j,) for j in range(2, N_TILES)]
 
@@ -450,6 +491,7 @@ def tile_tsh_mid_block_pb_kernel(
             add_bias_to_residual(j, nc.vector)
         for j in (0, 1):
             add_residual(j, 0)
+        add_bias_to_residual(2, nc.vector)
         transpose_h(2)
         for j in (0, 1):
             add_residual(j, 1)
@@ -463,7 +505,6 @@ def tile_tsh_mid_block_pb_kernel(
         for j in (0, 1):
             reciprocal(j)
             scale_and_shift(j)
-        add_bias_to_residual(2, side)
         first_matmul((2,), 0)
         quantise_h(3)
         add_residual(2, 0)
@@ -523,6 +564,6 @@ def tile_tsh_mid_block_pb_kernel(
         store(last - 2)
         second_matmul(last - 1)
         quantise_norm2(last, 2)
-        second_matmul(last)
+        second_matmul_in_halves(last)
         store(last - 1)
-        store(last)
+        store_halves(last)

@@ -69,7 +69,7 @@ def tile_tsh_mid_block_pb_kernel(
         shift = keep.tile([P, MID_PASSES, BANK], BF16)
         h_sb = {}
         res1_sb = {}
-        w_f2_sb = keep.tile([P, MID_PASSES, FFN_PASSES, BANK], U32, align_bytes=256)
+        w_f2_sb = keep.tile([P, FFN_PASSES, MID], U32, align_bytes=256)
         w_h_sb = keep.tile([P, MID_PASSES, D_OUT], U32, align_bytes=256)
 
         def load_h(j, pieces=1):
@@ -87,12 +87,10 @@ def tile_tsh_mid_block_pb_kernel(
             nc.sync.dma_start(out=res1_tile[:], in_=res1_rows[j * P : (j + 1) * P, :])
             res1_sb[j] = res1_tile
 
-        def load_w_f2(half, first, count):
+        def load_w_f2(first, count):
             nc.sync.dma_start(
-                out=w_f2_sb[:, half, first : first + count, :].bitcast(I32),
-                in_=w_f2_words[first : first + count]
-                .rearrange("g p n t -> p g (n t)")[:, :, half * BANK * PACK : (half + 1) * BANK * PACK]
-                .bitcast(I32),
+                out=w_f2_sb[:, first : first + count, :].bitcast(I32),
+                in_=w_f2_words[first : first + count].rearrange("g p n t -> p g (n t)").bitcast(I32),
             )
 
         def load_w_f2_scales(a):
@@ -122,17 +120,17 @@ def tile_tsh_mid_block_pb_kernel(
         load_h(0, 2)
         load_w_f2_scales(0)
         load_h(1, 2)
-        load_w_f2(0, 0, 2)
+        load_w_f2(0, 1)
         load_w_f2_scales(1)
-        load_w_f2(0, 2, 2)
-        load_w_f2(0, 4, 2)
-        load_w_f2(0, 6, 2)
+        load_w_f2(1, 1)
+        load_w_f2(2, 1)
+        load_w_f2(3, 1)
+        load_w_f2(4, 1)
         load_res1(0)
+        load_w_f2(5, 1)
         load_res1(1)
-        load_w_f2(1, 0, 2)
-        load_w_f2(1, 2, 2)
-        load_w_f2(1, 4, 2)
-        load_w_f2(1, 6, 2)
+        load_w_f2(6, 1)
+        load_w_f2(7, 1)
         load_res1(2)
         load_h(2, 2)
         load_h(3, 2)
@@ -239,11 +237,32 @@ def tile_tsh_mid_block_pb_kernel(
                         out=acc[(j, half)][:],
                         lhsT=h_codes[j][:, g * P : (g + 1) * P].bitcast(FP8X4),
                         lhsT_scale=h_planes[j][:, g * P : (g + 1) * P],
-                        rhs=w_f2_sb[:, half, g, :].bitcast(FP8X4),
+                        rhs=w_f2_sb[:, g, half * BANK : (half + 1) * BANK].bitcast(FP8X4),
                         rhs_scale=w_f2_planes[plane:P, g // PLANES_PER_TILE, half * BANK : (half + 1) * BANK],
                         start=(g == 0),
                         stop=(g == FFN_PASSES - 1),
                     )
+
+        def first_round():
+            for j in (0, 1):
+                bank = acc_pool.tile([P, BANK], F32, tag="acc")
+                acc[(j, 0)] = bank
+            for j in (0, 1):
+                bank = ring.tile([P, BANK], F32, tag="ring")
+                acc[(j, 1)] = bank
+            for g in range(FFN_PASSES):
+                plane = PACK * (g % PLANES_PER_TILE)
+                for j in (0, 1):
+                    for half in range(MID_PASSES):
+                        nc.tensor.matmul_mx(
+                            out=acc[(j, half)][:],
+                            lhsT=h_codes[j][:, g * P : (g + 1) * P].bitcast(FP8X4),
+                            lhsT_scale=h_planes[j][:, g * P : (g + 1) * P],
+                            rhs=w_f2_sb[:, g, half * BANK : (half + 1) * BANK].bitcast(FP8X4),
+                            rhs_scale=w_f2_planes[plane:P, g // PLANES_PER_TILE, half * BANK : (half + 1) * BANK],
+                            start=(g == 0),
+                            stop=(g == FFN_PASSES - 1),
+                        )
 
         def add_residual(j, half):
             if half == 0:
@@ -484,9 +503,8 @@ def tile_tsh_mid_block_pb_kernel(
             transpose_h(j)
             quantise_h(j)
         spread_b_f2()
-        first_matmul((0, 1), 0)
         spread_g2()
-        first_matmul((0, 1), 1, borrowed=True)
+        first_round()
         for j in (0, 1):
             add_bias_to_residual(j, nc.vector)
         for j in (0, 1):

@@ -243,14 +243,16 @@ def tile_tsh_mid_block_pb_kernel(
                         stop=(g == FFN_PASSES - 1),
                     )
 
-        def first_round():
+        def open_first_round():
             for j in (0, 1):
                 bank = acc_pool.tile([P, BANK], F32, tag="acc")
                 acc[(j, 0)] = bank
             for j in (0, 1):
                 bank = ring.tile([P, BANK], F32, tag="ring")
                 acc[(j, 1)] = bank
-            for g in range(FFN_PASSES):
+
+        def first_round_passes(first, end):
+            for g in range(first, end):
                 plane = PACK * (g % PLANES_PER_TILE)
                 for j in (0, 1):
                     for half in range(MID_PASSES):
@@ -498,23 +500,27 @@ def tile_tsh_mid_block_pb_kernel(
         def tiles(r):
             return rounds[r] if 0 <= r < len(rounds) else ()
 
-        side = nc.gpsimd if GP_BIAS else nc.vector
+        side = nc.vector
         for j in (0, 1):
             transpose_h(j)
             quantise_h(j)
         spread_b_f2()
+        open_first_round()
+        first_round_passes(0, 4)
         spread_g2()
-        first_round()
+        first_round_passes(4, FFN_PASSES)
         for j in (0, 1):
             add_bias_to_residual(j, nc.vector)
-        for j in (0, 1):
-            add_residual(j, 0)
-        add_bias_to_residual(2, nc.vector)
         transpose_h(2)
-        for j in (0, 1):
-            add_residual(j, 1)
-            mean(j)
-            deviation(j)
+        add_residual(0, 0)
+        add_residual(0, 1)
+        add_bias_to_residual(2, nc.vector)
+        mean(0)
+        deviation(0)
+        add_residual(1, 0)
+        add_residual(1, 1)
+        mean(1)
+        deviation(1)
         centre_and_gain(0)
         quantise_h(2)
         centre_and_gain(1)

@@ -297,6 +297,14 @@ def tile_tsh_mid_block_pb_kernel(
             )
             minus_mean[j] = negative
 
+        def mean_on_scalar(j):
+            negative = work.tile([P, 1], F32, tag="minus_mean", bufs=3)
+            scaled = work.tile([P, MID_PASSES], F32, tag="scaled_sums", bufs=2)
+            nc.scalar.activation(
+                out=scaled[:], in_=row_sums[j][:], func=ACT.Copy, scale=-1.0 / MID, accum_out=negative[:, 0:1]
+            )
+            minus_mean[j] = negative
+
         rstds = {}
         gained_rows = {}
 
@@ -538,15 +546,18 @@ def tile_tsh_mid_block_pb_kernel(
             for j in tiles(r + 3):
                 load_h(j)
                 load_res1(j)
+            if len(tiles(r - 3)) == 2:
+                for j in tiles(r - 3):
+                    store(j)
             for j in tiles(r - 1):
                 add_residual(j, 1)
-            for j in tiles(r - 3):
-                store(j)
-            for j in tiles(r - 1):
-                mean(j)
+            if len(tiles(r - 3)) == 1:
+                for j in tiles(r - 3):
+                    store(j)
             for j in tiles(r - 2):
                 transpose_norm2(j)
             for j in tiles(r - 1):
+                mean_on_scalar(j)
                 deviation(j)
             for j in tiles(r + 1):
                 add_bias_to_residual(j, side)

from contextlib import ExitStack

import concourse.mybir as mybir
from concourse.masks import make_identity

F32 = mybir.dt.float32
BF16 = mybir.dt.bfloat16
I32 = mybir.dt.int32
U32 = mybir.dt.uint32
U8 = mybir.dt.uint8
FP8X4 = mybir.dt.float8_e4m3fn_x4
ALU = mybir.AluOpType
ACT = mybir.ActivationFunctionType

P = 128
PACK = 4
K_PASS = P * PACK
BANK = 512
TOKENS = 1024
FFN = 4096
MID = 1024
D_OUT = 512
LN_EPS = 1e-5
N_TILES = TOKENS // P
FFN_PASSES = FFN // K_PASS
MID_PASSES = MID // K_PASS
PLANES_PER_TILE = 4
H_BUFFERS = 6
GP_BIAS = False
PSUM_CONST = False
FIRST_SORTED = 4

FLOPS = 2 * TOKENS * FFN * MID + 2 * TOKENS * MID * D_OUT


def tile_tsh_mid_block_pb_kernel(
    tc, h, w_f2_words, w_f2_scales, b_f2, res1, g2, be2, w_h_words, w_h_scales, b_h, out
):
    nc = tc.nc
    h_rows = h.flatten_outer_dims()
    res1_rows = res1.flatten_outer_dims()
    out_rows = out.flatten_outer_dims()

    with ExitStack() as ctx:
        ctx.enter_context(tc.manual_schedule())
        keep = ctx.enter_context(tc.tile_pool(name="keep", bufs=1))
        work = ctx.enter_context(tc.tile_pool(name="work", bufs=2))
        h_pool = ctx.enter_context(tc.tile_pool(name="h", bufs=H_BUFFERS))
        acc_pool = ctx.enter_context(tc.psum_pool(name="acc", bufs=2))
        ring = ctx.enter_context(tc.psum_pool(name="ring", bufs=4 if PSUM_CONST else 6))
        fixed = ctx.enter_context(tc.psum_pool(name="fixed", bufs=1)) if PSUM_CONST else None

        w_f2_planes = keep.tile([P, FFN_PASSES // PLANES_PER_TILE, MID], U8, align_bytes=256)
        nc.vector.memset(w_f2_planes[:].rearrange("q a n -> q (a n)").bitcast(I32), 0)
        vector_row = keep.tile([P, 3 * MID + D_OUT], BF16)
        nc.vector.memset(vector_row[:].bitcast(I32), 0)
        ones = keep.tile([P, P], BF16)
        nc.vector.memset(ones[:], 1.0)
        w_h_planes = keep.tile([P, D_OUT], U8, align_bytes=256)
        nc.vector.memset(w_h_planes[:].bitcast(I32), 0)
        eps = keep.tile([P, 1], F32)
        nc.vector.memset(eps[:], LN_EPS)
        ident_f32 = keep.tile([P, P], F32)
        make_identity(nc, ident_f32[:])

        bias_f2 = keep.tile([P, MID_PASSES, BANK], BF16)
        bias_h = keep.tile([P, D_OUT], BF16)
        gain = keep.tile([P, MID_PASSES, BANK], BF16)
        shift = keep.tile([P, MID_PASSES, BANK], BF16)
        h_sb = {}
        res1_sb = {}
        w_f2_sb = keep.tile([P, FFN_PASSES, MID], U32, align_bytes=256)
        w_h_sb = keep.tile([P, MID_PASSES, D_OUT], U32, align_bytes=256)

        def load_h(j, pieces=1):
            h_tile = h_pool.tile([P, FFN], BF16, tag="h")
            width = FFN // pieces
            for c in range(pieces):
                nc.sync.dma_start(
                    out=h_tile[:, c * width : (c + 1) * width],
                    in_=h_rows[j * P : (j + 1) * P, c * width : (c + 1) * width],
                )
            h_sb[j] = h_tile

        def load_res1(j):
            res1_tile = keep.tile([P, MID], BF16, name="res1_%d" % j)
            nc.sync.dma_start(out=res1_tile[:], in_=res1_rows[j * P : (j + 1) * P, :])
            res1_sb[j] = res1_tile

        def load_w_f2(first, count):
            nc.sync.dma_start(
                out=w_f2_sb[:, first : first + count, :].bitcast(I32),
                in_=w_f2_words[first : first + count].rearrange("g p n t -> p g (n t)").bitcast(I32),
            )

        def load_w_f2_scales(a):
            for quadrant in range(4):
                nc.sync.dma_start(
                    out=w_f2_planes[32 * quadrant : 32 * quadrant + 16, a, :].bitcast(I32),
                    in_=w_f2_scales[
                        PLANES_PER_TILE * a : PLANES_PER_TILE * (a + 1), 4 * quadrant : 4 * quadrant + 4, :
                    ].bitcast(I32),
                )

        def load_vector(v, vector):
            nc.gpsimd.dma_start(out=vector_row[0:1, v * MID : v * MID + vector.shape[0]], in_=vector.unsqueeze(0))

        def load_w_h():
            nc.sync.dma_start(
                out=w_h_sb[:].bitcast(I32), in_=w_h_words.rearrange("g p n t -> p g (n t)").bitcast(I32)
            )
            for quadrant in range(4):
                nc.sync.dma_start(
                    out=w_h_planes[32 * quadrant : 32 * quadrant + 4 * MID_PASSES, :].bitcast(I32),
                    in_=w_h_scales[:, 4 * quadrant : 4 * quadrant + 4, :].bitcast(I32),
                )

        load_vector(0, b_f2)
        load_vector(1, g2)
        load_h(0, 2)
        load_w_f2_scales(0)
        load_h(1, 2)
        load_w_f2(0, 1)
        load_w_f2_scales(1)
        load_w_f2(1, 1)
        load_w_f2(2, 1)
        load_w_f2(3, 1)
        load_w_f2(4, 1)
        load_res1(0)
        load_w_f2(5, 1)
        load_res1(1)
        load_w_f2(6, 1)
        load_w_f2(7, 1)
        load_res1(2)
        load_h(2, 2)
        load_h(3, 2)
        nc.sync.dma_start(out=shift[:].rearrange("q g n -> q (g n)"), in_=be2.partition_broadcast(P))
        load_h(4)
        load_w_h()
        nc.sync.dma_start(out=bias_h[:], in_=b_h.partition_broadcast(P))
        load_res1(3)
        load_res1(4)
        load_h(5)
        load_res1(5)


        def spread_vector(first, spread):
            bank = ring.tile([P, BANK], F32, tag="ring")
            nc.tensor.matmul(bank[:], lhsT=ones[:], rhs=vector_row[:, first : first + BANK], start=True, stop=True)
            nc.scalar.copy(out=spread, in_=bank[:])

        def spread_b_f2():
            for g in range(MID_PASSES):
                spread_vector(g * BANK, bias_f2[:, g])

        def spread_g2():
            for g in range(MID_PASSES):
                spread_vector(MID + g * BANK, gain[:, g])

        def spread_be2():
            for g in range(MID_PASSES):
                spread_vector(2 * MID + g * BANK, shift[:, g])

        def spread_b_h():
            spread_vector(3 * MID, bias_h[:])

        h_grouped = {}
        h_codes = {}
        h_planes = {}
        h_sorted = {}

        def h_words(j):
            return h_sb[j][:].bitcast(F32).rearrange("q (g p u) -> q g u p", g=FFN_PASSES, u=2)

        def sort_h(j):
            words = h_words(j)
            ordered = work.tile([P, FFN_PASSES, 2, P], F32, tag="h_sorted")
            for b in range(FFN_PASSES // 2):
                nc.scalar.copy(out=ordered[:, 2 * b : 2 * b + 2], in_=words[:, 2 * b : 2 * b + 2])
            h_sorted[j] = ordered

        def transpose_h(j):
            words = h_sorted[j][:] if j in h_sorted else h_words(j)
            grouped = work.tile([P, FFN], BF16, align_bytes=256, tag="h_grouped")
            grouped_words = grouped[:].bitcast(F32).rearrange("q (g c u) -> q g c u", g=FFN_PASSES, u=2)
            for b in range(FFN_PASSES // 2):
                bank = ring.tile([P, 2, 2, P], F32, tag="ring")
                for gg in range(2):
                    for u in range(2):
                        nc.tensor.transpose(bank[:, gg, u, :], words[:, 2 * b + gg, u, :], ident_f32[:])
                nc.scalar.copy(
                    out=grouped_words[:, 2 * b : 2 * b + 2, :, :],
                    in_=bank[:].rearrange("q g u c -> q g c u"),
                )
            h_grouped[j] = grouped

        def quantise_h(j, pieces=2):
            codes = work.tile([P, FFN_PASSES * P], U32, align_bytes=256, tag="h_codes", bufs=4)
            planes = work.tile([P, FFN_PASSES * P], U8, align_bytes=256, tag="h_planes", bufs=4)
            w = FFN_PASSES * P // pieces
            for a in range(pieces):
                nc.vector.quantize_mx(
                    out=codes[:, a * w : (a + 1) * w].bitcast(FP8X4),
                    scales=planes[:, a * w : (a + 1) * w],
                    in_=h_grouped[j][:, a * w * PACK : (a + 1) * w * PACK],
                )
            h_codes[j] = codes
            h_planes[j] = planes

        res1_biased = {}

        def add_bias_to_residual(j, engine):
            biased = work.tile([P, MID_PASSES, BANK], F32, tag="res1_biased", bufs=3)
            engine.tensor_tensor(
                out=biased[:].rearrange("q g n -> q (g n)"),
                in0=res1_sb[j][:],
                in1=bias_f2[:].rearrange("q g n -> q (g n)"),
                op=ALU.add,
            )
            res1_biased[j] = biased

        acc = {}
        res2 = {}
        row_sums = {}

        def first_matmul(group, half, borrowed=False):
            for j in group:
                if borrowed:
                    bank = ring.tile([P, BANK], F32, tag="ring")
                else:
                    bank = acc_pool.tile([P, BANK], F32, tag="acc")
                acc[(j, half)] = bank
            for g in range(FFN_PASSES):
                plane = PACK * (g % PLANES_PER_TILE)
                for j in group:
                    nc.tensor.matmul_mx(
                        out=acc[(j, half)][:],
                        lhsT=h_codes[j][:, g * P : (g + 1) * P].bitcast(FP8X4),
                        lhsT_scale=h_planes[j][:, g * P : (g + 1) * P],
                        rhs=w_f2_sb[:, g, half * BANK : (half + 1) * BANK].bitcast(FP8X4),
                        rhs_scale=w_f2_planes[plane:P, g // PLANES_PER_TILE, half * BANK : (half + 1) * BANK],
                        start=(g == 0),
                        stop=(g == FFN_PASSES - 1),
                    )

        def open_first_round():
            for j in (0, 1):
                bank = acc_pool.tile([P, BANK], F32, tag="acc")
                acc[(j, 0)] = bank
            for j in (0, 1):
                bank = ring.tile([P, BANK], F32, tag="ring")
                acc[(j, 1)] = bank

        def first_round_passes(first, end):
            for g in range(first, end):
                plane = PACK * (g % PLANES_PER_TILE)
                for j in (0, 1):
                    for half in range(MID_PASSES):
                        nc.tensor.matmul_mx(
                            out=acc[(j, half)][:],
                            lhsT=h_codes[j][:, g * P : (g + 1) * P].bitcast(FP8X4),
                            lhsT_scale=h_planes[j][:, g * P : (g + 1) * P],
                            rhs=w_f2_sb[:, g, half * BANK : (half + 1) * BANK].bitcast(FP8X4),
                            rhs_scale=w_f2_planes[plane:P, g // PLANES_PER_TILE, half * BANK : (half + 1) * BANK],
                            start=(g == 0),
                            stop=(g == FFN_PASSES - 1),
                        )

        def add_residual(j, half):
            if half == 0:
                res2_tile = work.tile([P, MID_PASSES, BANK], F32, tag="res2", bufs=3)
                res2[j] = res2_tile
                sums = work.tile([P, MID_PASSES], F32, tag="row_sums", bufs=3)
                row_sums[j] = sums
            nc.vector.scalar_tensor_tensor(
                out=res2[j][:, half],
                in0=acc[(j, half)][:],
                scalar=1.0,
                in1=res1_biased[j][:, half],
                op0=ALU.mult,
                op1=ALU.add,
                accum_out=row_sums[j][:, half : half + 1],
            )

        minus_mean = {}
        norm2_words = {}

        def mean(j):
            negative = work.tile([P, 1], F32, tag="minus_mean", bufs=3)
            nc.vector.tensor_scalar(
                out=negative[:],
                in0=row_sums[j][:, 0:1],
                scalar1=row_sums[j][:, 1:2],
                scalar2=-1.0 / MID,
                op0=ALU.add,
                op1=ALU.mult,
            )
            minus_mean[j] = negative

        def mean_on_scalar(j):
            negative = work.tile([P, 1], F32, tag="minus_mean", bufs=3)
            scaled = work.tile([P, MID_PASSES], F32, tag="scaled_sums", bufs=2)
            nc.scalar.activation(
                out=scaled[:], in_=row_sums[j][:], func=ACT.Copy, scale=-1.0 / MID, accum_out=negative[:, 0:1]
            )
            minus_mean[j] = negative

        rstds = {}
        gained_rows = {}

        def deviation(j):
            squares = work.tile([P, MID], BF16, tag="squares")
            sum_squares = work.tile([P, 1], F32, tag="sum_squares")
            nc.scalar.activation(
                out=squares[:],
                in_=res2[j][:].rearrange("q g n -> q (g n)"),
                func=ACT.Square,
                bias=minus_mean[j][:, 0:1],
                scale=1.0,
                accum_out=sum_squares[:, 0:1],
            )
            rstd = work.tile([P, 1], F32, tag="rstd", bufs=3)
            nc.scalar.activation(
                out=rstd[:], in_=sum_squares[:], func=ACT.Abs_reciprocal_sqrt, bias=eps[:, 0:1], scale=1.0 / MID
            )
            rstds[j] = rstd

        shifts = {}
        half_squares = {}

        def shift_of_half(j):
            shift_tile = work.tile([P, 2], F32, tag="half_shift", bufs=1)
            for column, sign in ((0, -1.0), (1, 1.0)):
                nc.scalar.activation(
                    out=shift_tile[:, column : column + 1],
                    in_=row_sums[j][:, 0:1],
                    func=ACT.Copy,
                    scale=sign / BANK,
                )
            shifts[j] = shift_tile

        def squares_of_half(j, half):
            squares = work.tile([P, MID], BF16, tag="squares")
            total = work.tile([P, 1], F32, tag="half_squares", bufs=2)
            nc.scalar.activation(
                out=squares[:, :BANK],
                in_=res2[j][:, half],
                func=ACT.Square,
                bias=shifts[j][:, 0:1],
                scale=1.0,
                accum_out=total[:, 0:1],
            )
            half_squares[(j, half)] = total

        def deviation_from_halves(j):
            offset = work.tile([P, 1], F32, tag="mean_offset", bufs=1)
            nc.scalar.activation(out=offset[:], in_=minus_mean[j][:], func=ACT.Square, bias=shifts[j][:, 1:2], scale=1.0)
            rest = work.tile([P, 1], F32, tag="variance_rest", bufs=1)
            nc.scalar.activation(
                out=rest[:], in_=offset[:], func=ACT.Identity, bias=first_half[j][:, 0:1], scale=-1.0
            )
            rstd = work.tile([P, 1], F32, tag="rstd", bufs=3)
            nc.scalar.activation(
                out=rstd[:],
                in_=half_squares[(j, 1)][:],
                func=ACT.Abs_reciprocal_sqrt,
                bias=rest[:, 0:1],
                scale=1.0 / MID,
            )
            rstds[j] = rstd

        first_half = {}

        def variance_of_first_half(j):
            part = work.tile([P, 1], F32, tag="first_half", bufs=1)
            nc.scalar.activation(
                out=part[:], in_=half_squares[(j, 0)][:], func=ACT.Identity, bias=eps[:, 0:1], scale=1.0 / MID
            )
            first_half[j] = part

        def centre_and_gain(j):
            gained = work.tile([P, MID], F32, tag="gained")
            nc.vector.scalar_tensor_tensor(
                out=gained[:],
                in0=res2[j][:].rearrange("q g n -> q (g n)"),
                scalar=minus_mean[j][:, 0:1],
                in1=gain[:].rearrange("q g n -> q (g n)"),
                op0=ALU.add,
                op1=ALU.mult,
            )
            gained_rows[j] = gained

        def reciprocal(j):
            return None

        def scale_and_shift(j, pieces=1):
            normed = work.tile([P, MID], BF16, tag="norm2", bufs=3)
            if j == N_TILES - 1:
                for g in range(MID_PASSES):
                    nc.vector.scalar_tensor_tensor(
                        out=normed[:, g * BANK : (g + 1) * BANK],
                        in0=gained_rows[j][:, g * BANK : (g + 1) * BANK],
                        scalar=rstds[j][:, 0:1],
                        in1=shift[:, g],
                        op0=ALU.mult,
                        op1=ALU.add,
                    )
                norm2_words[j] = normed[:].bitcast(F32).rearrange("q (g p u) -> q g u p", g=MID_PASSES, u=2)
            else:
                pairs = "q (x u e) -> q u x e"
                shift_pairs = shift[:].rearrange("q g n -> q (g n)").rearrange(pairs, u=2, e=2)
                for u in range(2):
                    nc.vector.scalar_tensor_tensor(
                        out=normed[:, u * BANK : (u + 1) * BANK].rearrange("q (x e) -> q x e", e=2),
                        in0=gained_rows[j][:].rearrange(pairs, u=2, e=2)[:, u],
                        scalar=rstds[j][:, 0:1],
                        in1=shift_pairs[:, u],
                        op0=ALU.mult,
                        op1=ALU.add,
                    )
                norm2_words[j] = normed[:].bitcast(F32).rearrange("q (u g p) -> q g u p", g=MID_PASSES, u=2)

        norm2_grouped = {}
        norm2_codes = {}
        norm2_planes = {}

        def transpose_norm2(j, pieces=1):
            words = norm2_words[j]
            grouped = work.tile([P, MID], BF16, align_bytes=256, tag="norm2_grouped")
            grouped_words = grouped[:].bitcast(F32).rearrange("q (g c u) -> q g c u", g=MID_PASSES, u=2)
            n = MID_PASSES // pieces
            for a in range(pieces):
                bank = ring.tile([P, n, 2, P], F32, tag="ring")
                for g in range(n):
                    for u in range(2):
                        nc.tensor.transpose(bank[:, g, u, :], words[:, a * n + g, u, :], ident_f32[:])
                nc.scalar.copy(
                    out=grouped_words[:, a * n : (a + 1) * n],
                    in_=bank[:].rearrange("q g u c -> q g c u"),
                )
            norm2_grouped[j] = grouped

        def quantise_norm2(j, pieces=1):
            codes = work.tile([P, MID_PASSES * P], U32, align_bytes=256, tag="norm2_codes")
            planes = work.tile([P, MID_PASSES * P], U8, align_bytes=256, tag="norm2_planes")
            w = MID_PASSES * P // pieces
            for a in range(pieces):
                nc.vector.quantize_mx(
                    out=codes[:, a * w : (a + 1) * w].bitcast(FP8X4),
                    scales=planes[:, a * w : (a + 1) * w],
                    in_=norm2_grouped[j][:, a * w * PACK : (a + 1) * w * PACK],
                )
            norm2_codes[j] = codes
            norm2_planes[j] = planes

        product = {}

        def second_matmul(j):
            bank = ring.tile([P, D_OUT], F32, tag="ring")
            for g in range(MID_PASSES):
                nc.tensor.matmul_mx(
                    out=bank[:],
                    lhsT=norm2_codes[j][:, g * P : (g + 1) * P].bitcast(FP8X4),
                    lhsT_scale=norm2_planes[j][:, g * P : (g + 1) * P],
                    rhs=w_h_sb[:, g, :].bitcast(FP8X4),
                    rhs_scale=w_h_planes[PACK * g : P, :],
                    start=(g == 0),
                    stop=(g == MID_PASSES - 1),
                )
            product[j] = bank

        def store(j):
            result = work.tile([P, D_OUT], F32, tag="result", bufs=4)
            nc.vector.tensor_tensor(out=result[:], in0=product[j][:], in1=bias_h[:], op=ALU.add)
            nc.sync.dma_start(out=out_rows[j * P : (j + 1) * P, :], in_=result[:])

        product_halves = []

        def second_matmul_in_halves(j):
            n = D_OUT // 2
            for c in range(2):
                bank = ring.tile([P, n], F32, tag="ring")
                product_halves.append(bank)
            for g in range(MID_PASSES):
                for c in range(2):
                    nc.tensor.matmul_mx(
                        out=product_halves[c][:],
                        lhsT=norm2_codes[j][:, g * P : (g + 1) * P].bitcast(FP8X4),
                        lhsT_scale=norm2_planes[j][:, g * P : (g + 1) * P],
                        rhs=w_h_sb[:, g, c * n : (c + 1) * n].bitcast(FP8X4),
                        rhs_scale=w_h_planes[PACK * g : P, c * n : (c + 1) * n],
                        start=(g == 0),
                        stop=(g == MID_PASSES - 1),
                    )

        def store_halves(j):
            n = D_OUT // 2
            for c in range(2):
                result = work.tile([P, n], F32, tag="result_half", bufs=2)
                nc.vector.tensor_tensor(
                    out=result[:], in0=product_halves[c][:], in1=bias_h[:, c * n : (c + 1) * n], op=ALU.add
                )
                nc.sync.dma_start(out=out_rows[j * P : (j + 1) * P, c * n : (c + 1) * n], in_=result[:])

        last = N_TILES - 1
        rounds = [(0, 1)] + [(j,) for j in range(2, N_TILES)]

        def tiles(r):
            return rounds[r] if 0 <= r < len(rounds) else ()

        side = nc.vector
        for j in (0, 1):
            transpose_h(j)
            quantise_h(j)
        spread_b_f2()
        open_first_round()
        first_round_passes(0, 4)
        spread_g2()
        first_round_passes(4, FFN_PASSES)
        for j in (0, 1):
            add_bias_to_residual(j, nc.vector)
        transpose_h(2)
        add_residual(0, 0)
        add_residual(0, 1)
        add_bias_to_residual(2, nc.vector)
        mean(0)
        deviation(0)
        add_residual(1, 0)
        add_residual(1, 1)
        mean(1)
        deviation(1)
        centre_and_gain(0)
        quantise_h(2)
        centre_and_gain(1)
        transpose_h(3)
        sort_h(4)
        for j in (0, 1):
            reciprocal(j)
            scale_and_shift(j)
        first_matmul((2,), 0)
        quantise_h(3)
        add_residual(2, 0)
        add_bias_to_residual(3, side)
        first_matmul((2,), 1)
        for r in range(2, len(rounds)):
            for j in tiles(r + 3):
                load_h(j)
                load_res1(j)
            if len(tiles(r - 3)) == 2:
                for j in tiles(r - 3):
                    store(j)
            for j in tiles(r - 1):
                add_residual(j, 1)
            if len(tiles(r - 3)) == 1:
                for j in tiles(r - 3):
                    store(j)
            for j in tiles(r - 2):
                transpose_norm2(j)
            for j in tiles(r - 1):
                mean_on_scalar(j)
                deviation(j)
            for j in tiles(r + 1):
                add_bias_to_residual(j, side)
            for j in tiles(r - 1):
                centre_and_gain(j)
            for j in tiles(r + 1):
                transpose_h(j)
            for j in tiles(r + 2):
                sort_h(j)
            for j in tiles(r):
                first_matmul((j,), 0)
            if r == len(rounds) - 1:
                add_residual(last, 0)
                shift_of_half(last)
                squares_of_half(last, 0)
                variance_of_first_half(last)
            for j in tiles(r - 2):
                quantise_norm2(j)
            for j in tiles(r - 1):
                scale_and_shift(j)
            if r < len(rounds) - 1:
                for j in tiles(r):
                    add_residual(j, 0)
            for j in tiles(r + 1):
                quantise_h(j, 1)
            for j in tiles(r):
                first_matmul((j,), 1)
            for j in tiles(r - 2):
                second_matmul(j)
        add_residual(last, 1)
        mean(last)
        squares_of_half(last, 1)
        deviation_from_halves(last)
        transpose_norm2(last - 1)
        centre_and_gain(last)
        scale_and_shift(last, 2)
        quantise_norm2(last - 1)
        transpose_norm2(last, 2)
        store(last - 2)
        second_matmul(last - 1)
        quantise_norm2(last, 2)
        second_matmul_in_halves(last)
        store(last - 1)
        store_halves(last)
